import numpy as np
import ml_dtypes


def mxq(x, axis, fmt="e4m3"):
    dtype, down = {"e4m3": (ml_dtypes.float8_e4m3fn, 7), "e5m2": (ml_dtypes.float8_e5m2, 14)}[fmt]
    v = np.moveaxis(np.asarray(x, np.float32).astype(ml_dtypes.bfloat16).astype(np.float64), axis, -1)
    blocks = v.reshape(v.shape[:-1] + (-1, 32))
    amax = np.abs(blocks).max(-1, keepdims=True)
    byte = np.maximum(np.where(amax > 0, np.frexp(amax)[1] - 1 + 127, 0) - down, 1)
    scale = np.exp2(byte - 127.0)
    codes = (blocks / scale).astype(np.float32).astype(dtype).astype(np.float64)
    return np.moveaxis((codes * scale).reshape(v.shape), -1, axis)


WIDE = False


def mx_kscale(k):
    if not WIDE:
        return np.ones(k)
    levels = np.array([10, -10, 5, -5, 0])
    if k % 512:
        return np.exp2(np.random.permutation(np.resize(levels, k // 32))).repeat(32)
    a = np.empty((k // 512, 16))
    for p in range(k // 512):
        a[p, :8] = np.random.permutation(np.resize(levels, 8))
        for g in range(8):
            far = levels[np.abs(levels - a[p, g]) >= 10]
            a[p, g + 8] = far[np.random.randint(len(far))]
    return np.exp2(a.ravel()).repeat(32)


BF16 = ml_dtypes.bfloat16


def bf(x):
    return np.asarray(x, np.float32).astype(BF16)


def f64(x):
    return np.asarray(x).astype(np.float64)


B, HEADS, CH, H, W, HSP, WSP = 2, 2, 256, 32, 64, 32, 32
C = HEADS * CH
U, V = H // HSP, W // WSP
NW = U * V
N = HSP * WSP


def _vid2win(x):
    x = x.reshape(B, HEADS, CH, U, HSP, V, WSP)
    x = x.transpose(0, 3, 5, 1, 4, 6, 2)
    return x.reshape(B * NW, HEADS, N, CH)


def setup_inputs():
    s = mx_kscale(N)
    sp = np.tile(s.reshape(HSP, WSP), (U, V))
    kv = np.random.standard_normal((2, B, C, H, W))
    kv[1] = kv[1] / sp * s.max()
    q = np.random.standard_normal((B, C, H, W)) * 1.5
    mask = np.random.standard_normal((NW, N, N)) + np.log(s)[None, None, :]
    return {"kv": bf(kv), "q": bf(q), "mask": bf(mask)}


def reference(kv, q, mask):
    kv = f64(kv)
    k, v = kv[0], kv[1]
    qw = _vid2win(f64(q))
    kw = _vid2win(k)
    vw = _vid2win(v)
    attn = (qw @ kw.transpose(0, 1, 3, 2)) * CH ** (-0.5)
    attn = attn.reshape(B, NW, HEADS, N, N) + f64(mask)[None, :, None]
    attn = attn.reshape(B * NW, HEADS, N, N)
    e = np.exp(attn - attn.max(-1, keepdims=True))
    x = (mxq(e, 3, "e4m3") @ mxq(vw, 2, "e4m3")) / e.sum(-1, keepdims=True)
    x = x.reshape(B, U, V, HEADS, HSP, WSP, CH)
    x = x.transpose(0, 3, 6, 1, 4, 2, 5)
    return x.reshape(B, C, H, W)

@@ -1,0 +1,382 @@
+from contextlib import ExitStack
+
+import concourse.mybir as mybir
+from concourse.masks import make_identity
+
+F32 = mybir.dt.float32
+BF16 = mybir.dt.bfloat16
+U32 = mybir.dt.uint32
+U8 = mybir.dt.uint8
+FP8X4 = mybir.dt.float8_e4m3fn_x4
+ALU = mybir.AluOpType
+ACT = mybir.ActivationFunctionType
+AX = mybir.AxisListType
+
+P = 128
+NKEY = 1024
+NT = 64
+FLOPS = 2 * 2 * 8 * 1024 * 1024 * 256
+
+MANUAL = True
+T_LAG = 5
+PE_MASK = (2, 7, 12)
+LAST_SPLIT = (2, 1, 1)
+
+
+def tile_window_attention_t_kernel(tc, kv, q, mask, out):
+    nc = tc.nc
+    with ExitStack() as ctx:
+        const = ctx.enter_context(tc.tile_pool(name="const", bufs=1))
+        maskp = ctx.enter_context(tc.tile_pool(name="maskp", bufs=1))
+        inp = ctx.enter_context(tc.tile_pool(name="inp", bufs=2))
+        work = ctx.enter_context(tc.tile_pool(name="work", bufs=2))
+        ps_s = ctx.enter_context(tc.psum_pool(name="ps_s", bufs=2))
+        ps_t = ctx.enter_context(tc.psum_pool(name="ps_t", bufs=2))
+        ps_o = ctx.enter_context(tc.psum_pool(name="ps_o", bufs=1))
+        if MANUAL:
+            ctx.enter_context(tc.manual_schedule())
+
+        ident_bf = const.tile([P, P], BF16, name="ident_bf")
+        make_identity(nc, ident_bf[:])
+        ident_f = const.tile([P, P], F32, name="ident_f")
+        make_identity(nc, ident_f[:])
+        ident16 = const.tile([P, P], BF16, name="ident16")
+        nc.vector.tensor_scalar_mul(out=ident16[:], in0=ident_bf[:], scalar1=16.0)
+
+        mask_sb = [maskp.tile([P, 8, NKEY], BF16, name="mask%d" % v) for v in range(2)]
+
+        groups = [(4 * h, 4) for h in range(15)]
+        first = 60
+        for n in LAST_SPLIT:
+            groups.append((first, n))
+            first += n
+        group_of = {}
+        for gi, (g0, gn) in enumerate(groups):
+            for i in range(g0, g0 + gn):
+                group_of[i] = gi
+        by_last = {}
+        for gi, (g0, gn) in enumerate(groups):
+            by_last[g0 + gn - 1] = gi
+
+        kraw = {}
+        qd = {}
+        vd = {}
+        oa = {}
+        vcode = {}
+        vscale = {}
+        gvt = {}
+        st = {}
+        ut = {}
+        nmt = {}
+        et = {}
+        xtt = {}
+        grp = {}
+        rst = {}
+        rt = {}
+        rsb = {}
+        ecode = {}
+        escale = {}
+        ot = {}
+
+        def chan0(pr, cc):
+            return (pr % 2) * 256 + cc * P
+
+        def alloc_k(pr, cc):
+            kraw[(pr, cc)] = inp.tile([P, 2048], BF16, name="kraw%d" % cc, tag="kraw%d" % cc)
+
+        def load_k(pr, cc, h0, h1):
+            c0 = chan0(pr, cc)
+            nc.sync.dma_start(
+                out=kraw[(pr, cc)][:, h0 * 64:h1 * 64],
+                in_=kv[0, pr // 2, c0:c0 + P, h0:h1, :].rearrange("c h w -> c (h w)"),
+            )
+
+        def alloc_win(store, label, pr, cc, v):
+            t = inp.tile([P, NKEY], BF16, name="%s%d%d" % (label, cc, v), tag="%s%d%d" % (label, cc, v))
+            store[(pr, cc, v)] = t
+
+        def load_win(store, src, pr, cc, v, h0, h1):
+            c0 = chan0(pr, cc)
+            t = store[(pr, cc, v)]
+            nc.sync.dma_start(
+                out=t[:, h0 * 32:h1 * 32].rearrange("c (h w) -> c h w", w=32),
+                in_=src[c0:c0 + P, h0:h1, v * 32:(v + 1) * 32],
+            )
+
+        def load_mask(v, t0, n):
+            nc.sync.dma_start(
+                out=mask_sb[v][:, t0:t0 + n, :],
+                in_=mask[v, t0 * P:(t0 + n) * P, :].rearrange("(t p) k -> p t k", p=P),
+            )
+
+        def load_pair(pr):
+            b = pr // 2
+            for cc in range(2):
+                alloc_k(pr, cc)
+                for v in range(2):
+                    alloc_win(qd, "qd", pr, cc, v)
+                    alloc_win(vd, "vd", pr, cc, v)
+            if pr == 0:
+                for cc in range(2):
+                    load_win(qd, q[b], pr, cc, 0, 0, 4)
+                for cc in range(2):
+                    load_k(pr, cc, 0, 16)
+                load_mask(0, 0, 1)
+                for cc in range(2):
+                    load_k(pr, cc, 16, 32)
+                for cc in range(2):
+                    load_win(qd, q[b], pr, cc, 0, 4, 16)
+                load_mask(0, 1, 1)
+                load_mask(0, 2, 2)
+                for cc in range(2):
+                    load_win(qd, q[b], pr, cc, 0, 16, 32)
+                load_mask(0, 4, 4)
+                for cc in range(2):
+                    load_win(vd, kv[1, b], pr, cc, 0, 0, 32)
+                for cc in range(2):
+                    load_win(qd, q[b], pr, cc, 1, 0, 32)
+                load_mask(1, 0, 4)
+                for cc in range(2):
+                    load_win(vd, kv[1, b], pr, cc, 1, 0, 32)
+                load_mask(1, 4, 4)
+            else:
+                for cc in range(2):
+                    load_k(pr, cc, 0, 32)
+                for v in range(2):
+                    for cc in range(2):
+                        load_win(qd, q[b], pr, cc, v, 0, 32)
+                    for cc in range(2):
+                        load_win(vd, kv[1, b], pr, cc, v, 0, 32)
+
+        def where(i):
+            inst = i // 8
+            return inst // 2, inst % 2, i % 8
+
+        def on_pe(i):
+            return i % 16 in PE_MASK
+
+        def scores(i, nh):
+            pr, v, qt = where(i)
+            s_nh = ps_s.tile([P, 512], F32, name="s%d" % nh, tag="s%d" % nh)
+            st[(i, nh)] = s_nh
+            for cc in range(2):
+                kview = kraw[(pr, cc)][:].rearrange("c (h v w) -> c h v w", v=2, w=32)
+                nc.tensor.matmul(
+                    out=s_nh[:].rearrange("p (h w) -> p h w", w=32),
+                    lhsT=qd[(pr, cc, v)][:, qt * P:(qt + 1) * P],
+                    rhs=kview[:, nh * 16:(nh + 1) * 16, v, :],
+                    start=(cc == 0),
+                    stop=(cc == 1 and not on_pe(i)),
+                )
+            if on_pe(i):
+                nc.tensor.matmul(
+                    out=s_nh[:],
+                    lhsT=ident16[:],
+                    rhs=mask_sb[v][:, qt, nh * 512:(nh + 1) * 512],
+                    start=False,
+                    stop=True,
+                )
+
+        def transposes(i, part):
+            if part == 0:
+                xtt[i] = ps_t.tile([P, 8, P], BF16, name="xt", tag="t")
+            for kb in range(4 * part, 4 * part + 4):
+                nc.tensor.transpose(out=xtt[i][:, kb, :], in_=et[i][:, kb * P:(kb + 1) * P], identity=ident_bf[:])
+
+        nm2t = {}
+
+        def leave_psum(i, nh):
+            pr, v, qt = where(i)
+            if nh == 0:
+                ut[i] = work.tile([P, NKEY], F32, name="u", tag="u", bufs=4)
+                if on_pe(i):
+                    nm2t[i] = work.tile([P, 2], F32, name="nm2", tag="nm2", bufs=2)
+            u = ut[i]
+            if on_pe(i):
+                nc.vector.tensor_scalar(
+                    out=u[:, nh * 512:(nh + 1) * 512].rearrange("q (t p) -> q t p", t=4),
+                    in0=st[(i, nh)][:].rearrange("q (p t) -> q t p", t=4),
+                    scalar1=-1.0 / 16.0,
+                    scalar2=None,
+                    op0=ALU.mult,
+                    op1=ALU.min,
+                    accum_out=nm2t[i][:, nh:nh + 1],
+                )
+            else:
+                nc.vector.scalar_tensor_tensor(
+                    out=u[:, nh * 512:(nh + 1) * 512].rearrange("q (t p) -> q t p", t=4),
+                    in0=st[(i, nh)][:].rearrange("q (p t) -> q t p", t=4),
+                    scalar=-1.0 / 16.0,
+                    in1=mask_sb[v][:, qt, nh * 512:(nh + 1) * 512].rearrange("q (p t) -> q t p", t=4),
+                    op0=ALU.mult,
+                    op1=ALU.subtract,
+                )
+
+        def row_min(i):
+            nm = work.tile([P, 1], F32, name="nm", tag="nm", bufs=5)
+            nmt[i] = nm
+            if on_pe(i):
+                nc.vector.tensor_tensor(out=nm[:], in0=nm2t[i][:, 0:1], in1=nm2t[i][:, 1:2], op=ALU.min)
+            else:
+                nc.vector.tensor_reduce(out=nm[:], in_=ut[i][:], axis=AX.X, op=ALU.min)
+
+        def exp_tile(i):
+            gi = group_of[i]
+            g0, gn = groups[gi]
+            if i == g0:
+                rst[gi] = work.tile([P, 4], F32, name="rs", tag="rs", bufs=4)
+            e = work.tile([P, NKEY], BF16, name="e", tag="e", bufs=T_LAG)
+            et[i] = e
+            nc.scalar.activation(
+                out=e[:], in_=ut[i][:], func=ACT.Exp, bias=nmt[i][:], scale=-1.0,
+                accum_out=rst[gi][:, i - g0:i - g0 + 1],
+            )
+
+        def evac_tile(i):
+            gi = group_of[i]
+            g0, gn = groups[gi]
+            jj = i - g0
+            if jj == 0:
+                grp[gi] = work.tile([P, 2, gn * P, 4], BF16, name="grp", tag="grp", bufs=2, align_bytes=64)
+            nc.scalar.copy(
+                out=grp[gi][:, :, jj * P:(jj + 1) * P, :],
+                in_=xtt[i][:].rearrange("p (g t) n -> p g n t", t=4),
+            )
+
+        def vpath_pe(inst):
+            pr, v = inst // 2, inst % 2
+            gvt[inst] = work.tile([P, 2, 256, 4], BF16, name="gv", tag="gv", bufs=2, align_bytes=64)
+            gwords = gvt[inst][:].rearrange("p g c t -> p (g c t)").bitcast(F32).rearrange("p (g c u) -> p g c u", g=2, u=2)
+            for cc in range(2):
+                vwords = vd[(pr, cc, v)][:].bitcast(F32)
+                vt = ps_t.tile([P, 4, P], F32, name="vt", tag="t")
+                for g in range(2):
+                    for uu in range(2):
+                        nc.tensor.transpose(out=vt[:, 2 * g + uu, :], in_=vwords[:, 256 * g + uu:256 * (g + 1):2], identity=ident_f[:])
+                nc.scalar.copy(
+                    out=gwords[:, :, cc * P:(cc + 1) * P, :],
+                    in_=vt[:].rearrange("p (g u) c -> p g c u", u=2),
+                )
+
+        def vpath_q(inst):
+            vcode[inst] = work.tile([P, 512], U32, name="vcode", tag="vcode", bufs=2, align_bytes=64)
+            vscale[inst] = work.tile([P, 512], U8, name="vscale", tag="vscale", bufs=2, align_bytes=64)
+            nc.vector.quantize_mx(
+                out=vcode[inst][:].bitcast(FP8X4),
+                scales=vscale[inst][:],
+                in_=gvt[inst][:].rearrange("p g c t -> p (g c t)"),
+            )
+
+        def recip(gi):
+            g0, gn = groups[gi]
+            rt[gi] = work.tile([P, 4], F32, name="r", tag="r", bufs=3)
+            nc.vector.reciprocal(out=rt[gi][:, 0:gn], in_=rst[gi][:, 0:gn])
+
+        def quant_e(gi):
+            g0, gn = groups[gi]
+            ecode[gi] = work.tile([P, 2 * gn * P], U32, name="ecode", tag="ecode", bufs=2, align_bytes=64)
+            escale[gi] = work.tile([P, 2 * gn * P], U8, name="escale", tag="escale", bufs=2, align_bytes=64)
+            nc.vector.quantize_mx(
+                out=ecode[gi][:].bitcast(FP8X4),
+                scales=escale[gi][:],
+                in_=grp[gi][:].rearrange("p g n t -> p (g n t)"),
+            )
+
+        def spread_r(gi):
+            g0, gn = groups[gi]
+            rp = ps_t.tile([P, gn * P], F32, name="rp", tag="t")
+            for jj in range(gn):
+                nc.tensor.transpose(
+                    out=rp[:, jj * P:(jj + 1) * P],
+                    in_=rt[gi][:, jj:jj + 1].to_broadcast([P, P]),
+                    identity=ident_f[:],
+                )
+            rsb[gi] = work.tile([P, gn * P], F32, name="rsb", tag="rsb", bufs=3)
+            nc.scalar.copy(out=rsb[gi][:], in_=rp[:])
+
+        def mx(gi):
+            g0, gn = groups[gi]
+            inst = g0 // 8
+            w = gn * P
+            o0 = ps_o.tile([P, w], F32, name="o0", tag="o0")
+            o1 = ps_o.tile([P, w], F32, name="o1", tag="o1")
+            ot[gi] = (o0, o1)
+            for cc in range(2):
+                for g in range(2):
+                    w0 = g * 256 + cc * P
+                    nc.tensor.matmul_mx(
+                        out=ot[gi][cc][:],
+                        lhsT=vcode[inst][:, w0:w0 + P].bitcast(FP8X4),
+                        lhsT_scale=vscale[inst][:, w0:w0 + P],
+                        rhs=ecode[gi][:, g * w:(g + 1) * w].bitcast(FP8X4),
+                        rhs_scale=escale[gi][:, g * w:(g + 1) * w],
+                        start=(g == 0),
+                        stop=(g == 1),
+                    )
+
+        def norm_store(gi, cc):
+            g0, gn = groups[gi]
+            pr, v, qt = where(g0)
+            h0, h1 = qt * 4, (qt + gn) * 4
+            if v == 0 and qt == 0:
+                oa[(pr, cc)] = work.tile([P, 32, 2, 32], F32, name="oa%d" % cc, tag="oa%d" % cc, bufs=2)
+            nc.vector.tensor_tensor(
+                out=oa[(pr, cc)][:, h0:h1, v, :],
+                in0=ot[gi][cc][:].rearrange("p (h w) -> p h w", w=32),
+                in1=rsb[gi][:].rearrange("p (h w) -> p h w", w=32),
+                op=ALU.mult,
+            )
+            if v == 1:
+                c0 = chan0(pr, cc)
+                nc.sync.dma_start(
+                    out=out[pr // 2, c0:c0 + P, h0:h1, :].rearrange("c h w -> c (h w)"),
+                    in_=oa[(pr, cc)][:, h0:h1, :, :].rearrange("c h v w -> c (h v w)"),
+                )
+
+        vpe_at = {6: 0}
+        vq_at = {8: 0}
+        for inst in range(1, 8):
+            vpe_at[8 * inst + 4] = inst
+            vq_at[8 * inst + 6] = inst
+
+        load_pair(0)
+        for s in range(NT + T_LAG + 8):
+            if s % 16 == 0 and s // 16 + 1 < 4:
+                load_pair(s // 16 + 1)
+            j = s - T_LAG
+            if s < NT:
+                scores(s, 0)
+            if 0 <= j < NT:
+                transposes(j, 0)
+            if s < NT:
+                scores(s, 1)
+            if j - 3 in by_last:
+                mx(by_last[j - 3])
+            if 0 <= j < NT:
+                transposes(j, 1)
+                evac_tile(j)
+            if s in vpe_at:
+                vpath_pe(vpe_at[s])
+            if j - 1 in by_last:
+                spread_r(by_last[j - 1])
+            if 0 <= s - 2 < NT:
+                exp_tile(s - 2)
+            if s < NT:
+                leave_psum(s, 0)
+            if 0 <= s - 1 < NT:
+                row_min(s - 1)
+            if s < NT:
+                leave_psum(s, 1)
+            if s in vq_at:
+                vpath_q(vq_at[s])
+            if s - 4 in by_last:
+                recip(by_last[s - 4])
+            if j - 1 in by_last:
+                quant_e(by_last[j - 1])
+            if j - 3 in by_last:
+                gi = by_last[j - 3]
+                norm_store(gi, 0)
+                if groups[gi][0] >= 60:
+                    norm_store(gi, 1)
+            if j - 4 in by_last and groups[by_last[j - 4]][0] < 60:
+                norm_store(by_last[j - 4], 1)

@@ -21,6 +21,7 @@ MANUAL = True
 T_LAG = 5
 PE_MASK = (2, 7, 12)
 LAST_SPLIT = (2, 1, 1)
+GP_UNTIL = 56
 
 
 def tile_window_attention_t_kernel(tc, kv, q, mask, out):
@@ -40,8 +41,8 @@ def tile_window_attention_t_kernel(tc, kv, q, mask, out):
         make_identity(nc, ident_bf[:])
         ident_f = const.tile([P, P], F32, name="ident_f")
         make_identity(nc, ident_f[:])
-        ident16 = const.tile([P, P], BF16, name="ident16")
-        nc.vector.tensor_scalar_mul(out=ident16[:], in0=ident_bf[:], scalar1=16.0)
+        identm = const.tile([P, P], BF16, name="identm")
+        nc.vector.tensor_scalar_mul(out=identm[:], in0=ident_bf[:], scalar1=-1.0)
 
         mask_sb = [maskp.tile([P, 8, NKEY], BF16, name="mask%d" % v) for v in range(2)]
 
@@ -60,6 +61,7 @@ def tile_window_attention_t_kernel(tc, kv, q, mask, out):
 
         kraw = {}
         qd = {}
+        qs = {}
         vd = {}
         oa = {}
         vcode = {}
@@ -103,6 +105,17 @@ def tile_window_attention_t_kernel(tc, kv, q, mask, out):
                 in_=src[c0:c0 + P, h0:h1, v * 32:(v + 1) * 32],
             )
 
+        def load_q(pr, cc, v, h0, h1):
+            load_win(qd, q[pr // 2], pr, cc, v, h0, h1)
+            nc.gpsimd.tensor_scalar(
+                out=qs[(pr, cc, v)][:, h0 * 32:h1 * 32],
+                in0=qd[(pr, cc, v)][:, h0 * 32:h1 * 32],
+                scalar1=-1.0 / 16.0,
+                scalar2=0.0,
+                op0=ALU.mult,
+                op1=ALU.add,
+            )
+
         def load_mask(v, t0, n):
             nc.sync.dma_start(
                 out=mask_sb[v][:, t0:t0 + n, :],
@@ -115,26 +128,27 @@ def tile_window_attention_t_kernel(tc, kv, q, mask, out):
                 alloc_k(pr, cc)
                 for v in range(2):
                     alloc_win(qd, "qd", pr, cc, v)
+                    alloc_win(qs, "qs", pr, cc, v)
                     alloc_win(vd, "vd", pr, cc, v)
             if pr == 0:
                 for cc in range(2):
-                    load_win(qd, q[b], pr, cc, 0, 0, 4)
+                    load_q(pr, cc, 0, 0, 4)
                 for cc in range(2):
                     load_k(pr, cc, 0, 16)
                 load_mask(0, 0, 1)
                 for cc in range(2):
                     load_k(pr, cc, 16, 32)
                 for cc in range(2):
-                    load_win(qd, q[b], pr, cc, 0, 4, 16)
+                    load_q(pr, cc, 0, 4, 16)
                 load_mask(0, 1, 1)
                 load_mask(0, 2, 2)
                 for cc in range(2):
-                    load_win(qd, q[b], pr, cc, 0, 16, 32)
+                    load_q(pr, cc, 0, 16, 32)
                 load_mask(0, 4, 4)
                 for cc in range(2):
                     load_win(vd, kv[1, b], pr, cc, 0, 0, 32)
                 for cc in range(2):
-                    load_win(qd, q[b], pr, cc, 1, 0, 32)
+                    load_q(pr, cc, 1, 0, 32)
                 load_mask(1, 0, 4)
                 for cc in range(2):
                     load_win(vd, kv[1, b], pr, cc, 1, 0, 32)
@@ -144,7 +158,7 @@ def tile_window_attention_t_kernel(tc, kv, q, mask, out):
                     load_k(pr, cc, 0, 32)
                 for v in range(2):
                     for cc in range(2):
-                        load_win(qd, q[b], pr, cc, v, 0, 32)
+                        load_q(pr, cc, v, 0, 32)
                     for cc in range(2):
                         load_win(vd, kv[1, b], pr, cc, v, 0, 32)
 
@@ -163,7 +177,7 @@ def tile_window_attention_t_kernel(tc, kv, q, mask, out):
                 kview = kraw[(pr, cc)][:].rearrange("c (h v w) -> c h v w", v=2, w=32)
                 nc.tensor.matmul(
                     out=s_nh[:].rearrange("p (h w) -> p h w", w=32),
-                    lhsT=qd[(pr, cc, v)][:, qt * P:(qt + 1) * P],
+                    lhsT=qs[(pr, cc, v)][:, qt * P:(qt + 1) * P],
                     rhs=kview[:, nh * 16:(nh + 1) * 16, v, :],
                     start=(cc == 0),
                     stop=(cc == 1 and not on_pe(i)),
@@ -171,7 +185,7 @@ def tile_window_attention_t_kernel(tc, kv, q, mask, out):
             if on_pe(i):
                 nc.tensor.matmul(
                     out=s_nh[:],
-                    lhsT=ident16[:],
+                    lhsT=identm[:],
                     rhs=mask_sb[v][:, qt, nh * 512:(nh + 1) * 512],
                     start=False,
                     stop=True,
@@ -179,9 +193,10 @@ def tile_window_attention_t_kernel(tc, kv, q, mask, out):
 
         def transposes(i, part):
             if part == 0:
-                xtt[i] = ps_t.tile([P, 8, P], BF16, name="xt", tag="t")
-            for kb in range(4 * part, 4 * part + 4):
-                nc.tensor.transpose(out=xtt[i][:, kb, :], in_=et[i][:, kb * P:(kb + 1) * P], identity=ident_bf[:])
+                xtt[i] = ps_t.tile([P, 4, P], F32, name="xt", tag="t")
+            ewords = et[i][:].bitcast(F32)
+            for kb in range(2 * part, 2 * part + 2):
+                nc.tensor.transpose(out=xtt[i][:, kb, :], in_=ewords[:, kb * P:(kb + 1) * P], identity=ident_f[:])
 
         nm2t = {}
 
@@ -194,22 +209,20 @@ def tile_window_attention_t_kernel(tc, kv, q, mask, out):
             u = ut[i]
             if on_pe(i):
                 nc.vector.tensor_scalar(
-                    out=u[:, nh * 512:(nh + 1) * 512].rearrange("q (t p) -> q t p", t=4),
-                    in0=st[(i, nh)][:].rearrange("q (p t) -> q t p", t=4),
-                    scalar1=-1.0 / 16.0,
+                    out=u[:, nh * 512:(nh + 1) * 512].rearrange("q (u p e) -> q u p e", u=2, e=2),
+                    in0=st[(i, nh)][:].rearrange("q (p u e) -> q u p e", u=2, e=2),
+                    scalar1=1.0,
                     scalar2=None,
                     op0=ALU.mult,
                     op1=ALU.min,
                     accum_out=nm2t[i][:, nh:nh + 1],
                 )
             else:
-                nc.vector.scalar_tensor_tensor(
-                    out=u[:, nh * 512:(nh + 1) * 512].rearrange("q (t p) -> q t p", t=4),
-                    in0=st[(i, nh)][:].rearrange("q (p t) -> q t p", t=4),
-                    scalar=-1.0 / 16.0,
-                    in1=mask_sb[v][:, qt, nh * 512:(nh + 1) * 512].rearrange("q (p t) -> q t p", t=4),
-                    op0=ALU.mult,
-                    op1=ALU.subtract,
+                nc.vector.tensor_tensor(
+                    out=u[:, nh * 512:(nh + 1) * 512].rearrange("q (u p e) -> q u p e", u=2, e=2),
+                    in0=st[(i, nh)][:].rearrange("q (p u e) -> q u p e", u=2, e=2),
+                    in1=mask_sb[v][:, qt, nh * 512:(nh + 1) * 512].rearrange("q (p u e) -> q u p e", u=2, e=2),
+                    op=ALU.subtract,
                 )
 
         def row_min(i):
@@ -238,9 +251,10 @@ def tile_window_attention_t_kernel(tc, kv, q, mask, out):
             jj = i - g0
             if jj == 0:
                 grp[gi] = work.tile([P, 2, gn * P, 4], BF16, name="grp", tag="grp", bufs=2, align_bytes=64)
+            gw = grp[gi][:].rearrange("p g n t -> p (g n t)").bitcast(F32).rearrange("p (g n u) -> p g n u", g=2, u=2)
             nc.scalar.copy(
-                out=grp[gi][:, :, jj * P:(jj + 1) * P, :],
-                in_=xtt[i][:].rearrange("p (g t) n -> p g n t", t=4),
+                out=gw[:, :, jj * P:(jj + 1) * P, :],
+                in_=xtt[i][:].rearrange("p (g u) n -> p g n u", u=2),
             )
 
         def vpath_pe(inst):
@@ -314,18 +328,36 @@ def tile_window_attention_t_kernel(tc, kv, q, mask, out):
                         stop=(g == 1),
                     )
 
+        osb = {}
+
+        def on_gp(gi):
+            return groups[gi][0] < GP_UNTIL
+
+        def o_out(gi, cc):
+            g0, gn = groups[gi]
+            osb[(gi, cc)] = work.tile([P, gn * P], F32, name="osb%d" % cc, tag="osb%d" % cc, bufs=2)
+            nc.scalar.copy(out=osb[(gi, cc)][:], in_=ot[gi][cc][:])
+
         def norm_store(gi, cc):
             g0, gn = groups[gi]
             pr, v, qt = where(g0)
             h0, h1 = qt * 4, (qt + gn) * 4
             if v == 0 and qt == 0:
                 oa[(pr, cc)] = work.tile([P, 32, 2, 32], F32, name="oa%d" % cc, tag="oa%d" % cc, bufs=2)
-            nc.vector.tensor_tensor(
-                out=oa[(pr, cc)][:, h0:h1, v, :],
-                in0=ot[gi][cc][:].rearrange("p (h w) -> p h w", w=32),
-                in1=rsb[gi][:].rearrange("p (h w) -> p h w", w=32),
-                op=ALU.mult,
-            )
+            if on_gp(gi):
+                nc.gpsimd.tensor_tensor(
+                    out=oa[(pr, cc)][:, h0:h1, v, :],
+                    in0=osb[(gi, cc)][:].rearrange("p (h w) -> p h w", w=32),
+                    in1=rsb[gi][:].rearrange("p (h w) -> p h w", w=32),
+                    op=ALU.mult,
+                )
+            else:
+                nc.vector.tensor_tensor(
+                    out=oa[(pr, cc)][:, h0:h1, v, :],
+                    in0=ot[gi][cc][:].rearrange("p (h w) -> p h w", w=32),
+                    in1=rsb[gi][:].rearrange("p (h w) -> p h w", w=32),
+                    op=ALU.mult,
+                )
             if v == 1:
                 c0 = chan0(pr, cc)
                 nc.sync.dma_start(
@@ -361,6 +393,9 @@ def tile_window_attention_t_kernel(tc, kv, q, mask, out):
                 spread_r(by_last[j - 1])
             if 0 <= s - 2 < NT:
                 exp_tile(s - 2)
+            if j - 3 in by_last and on_gp(by_last[j - 3]):
+                o_out(by_last[j - 3], 0)
+                o_out(by_last[j - 3], 1)
             if s < NT:
                 leave_psum(s, 0)
             if 0 <= s - 1 < NT:
@@ -376,7 +411,7 @@ def tile_window_attention_t_kernel(tc, kv, q, mask, out):
             if j - 3 in by_last:
                 gi = by_last[j - 3]
                 norm_store(gi, 0)
-                if groups[gi][0] >= 60:
+                if groups[gi][0] >= 60 or on_gp(gi):
                     norm_store(gi, 1)
-            if j - 4 in by_last and groups[by_last[j - 4]][0] < 60:
+            if j - 4 in by_last and groups[by_last[j - 4]][0] < 60 and not on_gp(by_last[j - 4]):
                 norm_store(by_last[j - 4], 1)

@@ -105,11 +105,18 @@ def tile_window_attention_t_kernel(tc, kv, q, mask, out):
                 in_=src[c0:c0 + P, h0:h1, v * 32:(v + 1) * 32],
             )
 
-        def load_q(pr, cc, v, h0, h1):
-            load_win(qd, q[pr // 2], pr, cc, v, h0, h1)
+        def load_q(pr, cc, h0, h1):
+            c0 = chan0(pr, cc)
+            nc.sync.dma_start(
+                out=qd[(pr, cc)][:, h0 * 64:h1 * 64],
+                in_=q[pr // 2, c0:c0 + P, h0:h1, :].rearrange("c h w -> c (h w)"),
+            )
+
+        def scale_q(pr, cc, v, h0, h1):
+            qview = qd[(pr, cc)][:].rearrange("c (h v w) -> c h v w", v=2, w=32)
             nc.gpsimd.tensor_scalar(
-                out=qs[(pr, cc, v)][:, h0 * 32:h1 * 32],
-                in0=qd[(pr, cc, v)][:, h0 * 32:h1 * 32],
+                out=qs[(pr, cc, v)][:, h0 * 32:h1 * 32].rearrange("c (h w) -> c h w", w=32),
+                in0=qview[:, h0:h1, v, :],
                 scalar1=-1.0 / 16.0,
                 scalar2=0.0,
                 op0=ALU.mult,
@@ -126,29 +133,32 @@ def tile_window_attention_t_kernel(tc, kv, q, mask, out):
             b = pr // 2
             for cc in range(2):
                 alloc_k(pr, cc)
+                qd[(pr, cc)] = inp.tile([P, 2048], BF16, name="qd%d" % cc, tag="qd%d" % cc)
                 for v in range(2):
-                    alloc_win(qd, "qd", pr, cc, v)
                     alloc_win(qs, "qs", pr, cc, v)
                     alloc_win(vd, "vd", pr, cc, v)
             if pr == 0:
                 for cc in range(2):
-                    load_q(pr, cc, 0, 0, 4)
+                    load_q(pr, cc, 0, 4)
+                    scale_q(pr, cc, 0, 0, 4)
                 for cc in range(2):
                     load_k(pr, cc, 0, 16)
                 load_mask(0, 0, 1)
                 for cc in range(2):
                     load_k(pr, cc, 16, 32)
                 for cc in range(2):
-                    load_q(pr, cc, 0, 4, 16)
+                    load_q(pr, cc, 4, 16)
+                    scale_q(pr, cc, 0, 4, 16)
                 load_mask(0, 1, 1)
                 load_mask(0, 2, 2)
                 for cc in range(2):
-                    load_q(pr, cc, 0, 16, 32)
+                    load_q(pr, cc, 16, 32)
+                    scale_q(pr, cc, 0, 16, 32)
                 load_mask(0, 4, 4)
                 for cc in range(2):
                     load_win(vd, kv[1, b], pr, cc, 0, 0, 32)
                 for cc in range(2):
-                    load_q(pr, cc, 1, 0, 32)
+                    scale_q(pr, cc, 1, 0, 32)
                 load_mask(1, 0, 4)
                 for cc in range(2):
                     load_win(vd, kv[1, b], pr, cc, 1, 0, 32)
@@ -156,9 +166,9 @@ def tile_window_attention_t_kernel(tc, kv, q, mask, out):
             else:
                 for cc in range(2):
                     load_k(pr, cc, 0, 32)
+                for cc in range(2):
+                    load_q(pr, cc, 0, 32)
                 for v in range(2):
-                    for cc in range(2):
-                        load_q(pr, cc, v, 0, 32)
                     for cc in range(2):
                         load_win(vd, kv[1, b], pr, cc, v, 0, 32)
 
@@ -415,3 +425,5 @@ def tile_window_attention_t_kernel(tc, kv, q, mask, out):
                     norm_store(gi, 1)
             if j - 4 in by_last and groups[by_last[j - 4]][0] < 60 and not on_gp(by_last[j - 4]):
                 norm_store(by_last[j - 4], 1)
+            if 8 <= s % 16 < 12 and s // 16 + 1 < 4:
+                scale_q(s // 16 + 1, (s % 16 - 8) % 2, (s % 16 - 8) // 2, 0, 32)

@@ -17,11 +17,23 @@ NKEY = 1024
 NT = 64
 FLOPS = 2 * 2 * 8 * 1024 * 1024 * 256
 
-MANUAL = True
 T_LAG = 5
+E_BUFS = 5
+U_BUFS = 4
 PE_MASK = (2, 7, 12)
+AR_SET = ()
 LAST_SPLIT = (2, 1, 1)
 GP_UNTIL = 56
+D_QE = 6
+D_RC = 4
+D_RS = 6
+D_MX = (8, 9)
+D_O = (8, 9)
+D_M = (8, 9)
+D_VT = (0, 4)
+D_QV = 6
+D_SQ = (8, 9, 10, 11)
+T_BUFS = 2
 
 
 def tile_window_attention_t_kernel(tc, kv, q, mask, out):
@@ -32,10 +44,9 @@ def tile_window_attention_t_kernel(tc, kv, q, mask, out):
         inp = ctx.enter_context(tc.tile_pool(name="inp", bufs=2))
         work = ctx.enter_context(tc.tile_pool(name="work", bufs=2))
         ps_s = ctx.enter_context(tc.psum_pool(name="ps_s", bufs=2))
-        ps_t = ctx.enter_context(tc.psum_pool(name="ps_t", bufs=2))
+        ps_t = ctx.enter_context(tc.psum_pool(name="ps_t", bufs=T_BUFS))
         ps_o = ctx.enter_context(tc.psum_pool(name="ps_o", bufs=1))
-        if MANUAL:
-            ctx.enter_context(tc.manual_schedule())
+        ctx.enter_context(tc.manual_schedule())
 
         ident_bf = const.tile([P, P], BF16, name="ident_bf")
         make_identity(nc, ident_bf[:])
@@ -70,6 +81,7 @@ def tile_window_attention_t_kernel(tc, kv, q, mask, out):
         st = {}
         ut = {}
         nmt = {}
+        nm2t = {}
         et = {}
         xtt = {}
         grp = {}
@@ -79,37 +91,30 @@ def tile_window_attention_t_kernel(tc, kv, q, mask, out):
         ecode = {}
         escale = {}
         ot = {}
+        osb = {}
+        tqt = {}
 
         def chan0(pr, cc):
             return (pr % 2) * 256 + cc * P
 
-        def alloc_k(pr, cc):
-            kraw[(pr, cc)] = inp.tile([P, 2048], BF16, name="kraw%d" % cc, tag="kraw%d" % cc)
+        def load_rows(t, src, pr, cc, h0, h1):
+            c0 = chan0(pr, cc)
+            nc.sync.dma_start(
+                out=t[:, h0 * 64:h1 * 64],
+                in_=src[c0:c0 + P, h0:h1, :].rearrange("c h w -> c (h w)"),
+            )
 
         def load_k(pr, cc, h0, h1):
-            c0 = chan0(pr, cc)
-            nc.sync.dma_start(
-                out=kraw[(pr, cc)][:, h0 * 64:h1 * 64],
-                in_=kv[0, pr // 2, c0:c0 + P, h0:h1, :].rearrange("c h w -> c (h w)"),
-            )
-
-        def alloc_win(store, label, pr, cc, v):
-            t = inp.tile([P, NKEY], BF16, name="%s%d%d" % (label, cc, v), tag="%s%d%d" % (label, cc, v))
-            store[(pr, cc, v)] = t
-
-        def load_win(store, src, pr, cc, v, h0, h1):
-            c0 = chan0(pr, cc)
-            t = store[(pr, cc, v)]
-            nc.sync.dma_start(
-                out=t[:, h0 * 32:h1 * 32].rearrange("c (h w) -> c h w", w=32),
-                in_=src[c0:c0 + P, h0:h1, v * 32:(v + 1) * 32],
-            )
+            load_rows(kraw[(pr, cc)], kv[0, pr // 2], pr, cc, h0, h1)
 
         def load_q(pr, cc, h0, h1):
+            load_rows(qd[(pr, cc)], q[pr // 2], pr, cc, h0, h1)
+
+        def load_v(pr, cc, v):
             c0 = chan0(pr, cc)
             nc.sync.dma_start(
-                out=qd[(pr, cc)][:, h0 * 64:h1 * 64],
-                in_=q[pr // 2, c0:c0 + P, h0:h1, :].rearrange("c h w -> c (h w)"),
+                out=vd[(pr, cc, v)][:].rearrange("c (h w) -> c h w", w=32),
+                in_=kv[1, pr // 2, c0:c0 + P, :, v * 32:(v + 1) * 32],
             )
 
         def scale_q(pr, cc, v, h0, h1):
@@ -130,13 +135,12 @@ def tile_window_attention_t_kernel(tc, kv, q, mask, out):
             )
 
         def load_pair(pr):
-            b = pr // 2
             for cc in range(2):
-                alloc_k(pr, cc)
+                kraw[(pr, cc)] = inp.tile([P, 2048], BF16, name="kraw%d" % cc, tag="kraw%d" % cc)
                 qd[(pr, cc)] = inp.tile([P, 2048], BF16, name="qd%d" % cc, tag="qd%d" % cc)
                 for v in range(2):
-                    alloc_win(qs, "qs", pr, cc, v)
-                    alloc_win(vd, "vd", pr, cc, v)
+                    qs[(pr, cc, v)] = inp.tile([P, NKEY], BF16, name="qs%d%d" % (cc, v), tag="qs%d%d" % (cc, v))
+                    vd[(pr, cc, v)] = inp.tile([P, NKEY], BF16, name="vd%d%d" % (cc, v), tag="vd%d%d" % (cc, v))
             if pr == 0:
                 for cc in range(2):
                     load_q(pr, cc, 0, 4)
@@ -156,12 +160,12 @@ def tile_window_attention_t_kernel(tc, kv, q, mask, out):
                     scale_q(pr, cc, 0, 16, 32)
                 load_mask(0, 4, 4)
                 for cc in range(2):
-                    load_win(vd, kv[1, b], pr, cc, 0, 0, 32)
+                    load_v(pr, cc, 0)
                 for cc in range(2):
                     scale_q(pr, cc, 1, 0, 32)
                 load_mask(1, 0, 4)
                 for cc in range(2):
-                    load_win(vd, kv[1, b], pr, cc, 1, 0, 32)
+                    load_v(pr, cc, 1)
                 load_mask(1, 4, 4)
             else:
                 for cc in range(2):
@@ -170,7 +174,7 @@ def tile_window_attention_t_kernel(tc, kv, q, mask, out):
                     load_q(pr, cc, 0, 32)
                 for v in range(2):
                     for cc in range(2):
-                        load_win(vd, kv[1, b], pr, cc, v, 0, 32)
+                        load_v(pr, cc, v)
 
         def where(i):
             inst = i // 8
@@ -178,6 +182,18 @@ def tile_window_attention_t_kernel(tc, kv, q, mask, out):
 
         def on_pe(i):
             return i % 16 in PE_MASK
+
+        def on_ar(i):
+            return i % 16 in AR_SET
+
+        def perm(ap):
+            return ap.rearrange("q (p u e) -> q u p e", u=2, e=2)
+
+        def flat(ap):
+            return ap.rearrange("q (u p e) -> q u p e", u=2, e=2)
+
+        def half(nh):
+            return slice(nh * 512, (nh + 1) * 512)
 
         def scores(i, nh):
             pr, v, qt = where(i)
@@ -193,13 +209,7 @@ def tile_window_attention_t_kernel(tc, kv, q, mask, out):
                     stop=(cc == 1 and not on_pe(i)),
                 )
             if on_pe(i):
-                nc.tensor.matmul(
-                    out=s_nh[:],
-                    lhsT=identm[:],
-                    rhs=mask_sb[v][:, qt, nh * 512:(nh + 1) * 512],
-                    start=False,
-                    stop=True,
-                )
+                nc.tensor.matmul(out=s_nh[:], lhsT=identm[:], rhs=mask_sb[v][:, qt, half(nh)], start=False, stop=True)
 
         def transposes(i, part):
             if part == 0:
@@ -208,35 +218,40 @@ def tile_window_attention_t_kernel(tc, kv, q, mask, out):
             for kb in range(2 * part, 2 * part + 2):
                 nc.tensor.transpose(out=xtt[i][:, kb, :], in_=ewords[:, kb * P:(kb + 1) * P], identity=ident_f[:])
 
-        nm2t = {}
-
         def leave_psum(i, nh):
             pr, v, qt = where(i)
             if nh == 0:
-                ut[i] = work.tile([P, NKEY], F32, name="u", tag="u", bufs=4)
+                ut[i] = work.tile([P, NKEY], F32, name="u", tag="u", bufs=U_BUFS)
                 if on_pe(i):
                     nm2t[i] = work.tile([P, 2], F32, name="nm2", tag="nm2", bufs=2)
             u = ut[i]
             if on_pe(i):
                 nc.vector.tensor_scalar(
-                    out=u[:, nh * 512:(nh + 1) * 512].rearrange("q (u p e) -> q u p e", u=2, e=2),
-                    in0=st[(i, nh)][:].rearrange("q (p u e) -> q u p e", u=2, e=2),
-                    scalar1=1.0,
-                    scalar2=None,
-                    op0=ALU.mult,
-                    op1=ALU.min,
-                    accum_out=nm2t[i][:, nh:nh + 1],
+                    out=flat(u[:, half(nh)]), in0=perm(st[(i, nh)][:]), scalar1=1.0, scalar2=None,
+                    op0=ALU.mult, op1=ALU.min, accum_out=nm2t[i][:, nh:nh + 1],
                 )
             else:
                 nc.vector.tensor_tensor(
-                    out=u[:, nh * 512:(nh + 1) * 512].rearrange("q (u p e) -> q u p e", u=2, e=2),
-                    in0=st[(i, nh)][:].rearrange("q (p u e) -> q u p e", u=2, e=2),
-                    in1=mask_sb[v][:, qt, nh * 512:(nh + 1) * 512].rearrange("q (p u e) -> q u p e", u=2, e=2),
+                    out=flat(u[:, half(nh)]), in0=perm(st[(i, nh)][:]), in1=perm(mask_sb[v][:, qt, half(nh)]),
                     op=ALU.subtract,
                 )
 
+        def ar_copy(i, nh):
+            if nh == 0:
+                tqt[i] = work.tile([P, NKEY], F32, name="tq", tag="tq", bufs=2)
+            nc.scalar.copy(out=flat(tqt[i][:, half(nh)]), in_=perm(st[(i, nh)][:]))
+
+        def ar_add(i, nh):
+            pr, v, qt = where(i)
+            if nh == 0:
+                ut[i] = work.tile([P, NKEY], F32, name="ua", tag="ua", bufs=2)
+            nc.gpsimd.tensor_tensor(
+                out=flat(ut[i][:, half(nh)]), in0=flat(tqt[i][:, half(nh)]), in1=perm(mask_sb[v][:, qt, half(nh)]),
+                op=ALU.subtract,
+            )
+
         def row_min(i):
-            nm = work.tile([P, 1], F32, name="nm", tag="nm", bufs=5)
+            nm = work.tile([P, 1], F32, name="nm", tag="nm", bufs=6)
             nmt[i] = nm
             if on_pe(i):
                 nc.vector.tensor_tensor(out=nm[:], in0=nm2t[i][:, 0:1], in1=nm2t[i][:, 1:2], op=ALU.min)
@@ -248,7 +263,7 @@ def tile_window_attention_t_kernel(tc, kv, q, mask, out):
             g0, gn = groups[gi]
             if i == g0:
                 rst[gi] = work.tile([P, 4], F32, name="rs", tag="rs", bufs=4)
-            e = work.tile([P, NKEY], BF16, name="e", tag="e", bufs=T_LAG)
+            e = work.tile([P, NKEY], BF16, name="e", tag="e", bufs=E_BUFS)
             et[i] = e
             nc.scalar.activation(
                 out=e[:], in_=ut[i][:], func=ACT.Exp, bias=nmt[i][:], scale=-1.0,
@@ -267,20 +282,20 @@ def tile_window_attention_t_kernel(tc, kv, q, mask, out):
                 in_=xtt[i][:].rearrange("p (g u) n -> p g n u", u=2),
             )
 
-        def vpath_pe(inst):
+        def vpath_pe(inst, cc):
             pr, v = inst // 2, inst % 2
-            gvt[inst] = work.tile([P, 2, 256, 4], BF16, name="gv", tag="gv", bufs=2, align_bytes=64)
+            if inst not in gvt:
+                gvt[inst] = work.tile([P, 2, 256, 4], BF16, name="gv", tag="gv", bufs=2, align_bytes=64)
             gwords = gvt[inst][:].rearrange("p g c t -> p (g c t)").bitcast(F32).rearrange("p (g c u) -> p g c u", g=2, u=2)
-            for cc in range(2):
-                vwords = vd[(pr, cc, v)][:].bitcast(F32)
-                vt = ps_t.tile([P, 4, P], F32, name="vt", tag="t")
-                for g in range(2):
-                    for uu in range(2):
-                        nc.tensor.transpose(out=vt[:, 2 * g + uu, :], in_=vwords[:, 256 * g + uu:256 * (g + 1):2], identity=ident_f[:])
-                nc.scalar.copy(
-                    out=gwords[:, :, cc * P:(cc + 1) * P, :],
-                    in_=vt[:].rearrange("p (g u) c -> p g c u", u=2),
-                )
+            vwords = vd[(pr, cc, v)][:].bitcast(F32)
+            vt = ps_t.tile([P, 4, P], F32, name="vt", tag="t")
+            for g in range(2):
+                for uu in range(2):
+                    nc.tensor.transpose(out=vt[:, 2 * g + uu, :], in_=vwords[:, 256 * g + uu:256 * (g + 1):2], identity=ident_f[:])
+            nc.scalar.copy(
+                out=gwords[:, :, cc * P:(cc + 1) * P, :],
+                in_=vt[:].rearrange("p (g u) c -> p g c u", u=2),
+            )
 
         def vpath_q(inst):
             vcode[inst] = work.tile([P, 512], U32, name="vcode", tag="vcode", bufs=2, align_bytes=64)
@@ -318,27 +333,22 @@ def tile_window_attention_t_kernel(tc, kv, q, mask, out):
             rsb[gi] = work.tile([P, gn * P], F32, name="rsb", tag="rsb", bufs=3)
             nc.scalar.copy(out=rsb[gi][:], in_=rp[:])
 
-        def mx(gi):
+        def mx(gi, cc):
             g0, gn = groups[gi]
             inst = g0 // 8
             w = gn * P
-            o0 = ps_o.tile([P, w], F32, name="o0", tag="o0")
-            o1 = ps_o.tile([P, w], F32, name="o1", tag="o1")
-            ot[gi] = (o0, o1)
-            for cc in range(2):
-                for g in range(2):
-                    w0 = g * 256 + cc * P
-                    nc.tensor.matmul_mx(
-                        out=ot[gi][cc][:],
-                        lhsT=vcode[inst][:, w0:w0 + P].bitcast(FP8X4),
-                        lhsT_scale=vscale[inst][:, w0:w0 + P],
-                        rhs=ecode[gi][:, g * w:(g + 1) * w].bitcast(FP8X4),
-                        rhs_scale=escale[gi][:, g * w:(g + 1) * w],
-                        start=(g == 0),
-                        stop=(g == 1),
-                    )
-
-        osb = {}
+            ot[(gi, cc)] = ps_o.tile([P, w], F32, name="o%d" % cc, tag="o%d" % cc)
+            for g in range(2):
+                w0 = g * 256 + cc * P
+                nc.tensor.matmul_mx(
+                    out=ot[(gi, cc)][:],
+                    lhsT=vcode[inst][:, w0:w0 + P].bitcast(FP8X4),
+                    lhsT_scale=vscale[inst][:, w0:w0 + P],
+                    rhs=ecode[gi][:, g * w:(g + 1) * w].bitcast(FP8X4),
+                    rhs_scale=escale[gi][:, g * w:(g + 1) * w],
+                    start=(g == 0),
+                    stop=(g == 1),
+                )
 
         def on_gp(gi):
             return groups[gi][0] < GP_UNTIL
@@ -346,7 +356,7 @@ def tile_window_attention_t_kernel(tc, kv, q, mask, out):
         def o_out(gi, cc):
             g0, gn = groups[gi]
             osb[(gi, cc)] = work.tile([P, gn * P], F32, name="osb%d" % cc, tag="osb%d" % cc, bufs=2)
-            nc.scalar.copy(out=osb[(gi, cc)][:], in_=ot[gi][cc][:])
+            nc.scalar.copy(out=osb[(gi, cc)][:], in_=ot[(gi, cc)][:])
 
         def norm_store(gi, cc):
             g0, gn = groups[gi]
@@ -364,7 +374,7 @@ def tile_window_attention_t_kernel(tc, kv, q, mask, out):
             else:
                 nc.vector.tensor_tensor(
                     out=oa[(pr, cc)][:, h0:h1, v, :],
-                    in0=ot[gi][cc][:].rearrange("p (h w) -> p h w", w=32),
+                    in0=ot[(gi, cc)][:].rearrange("p (h w) -> p h w", w=32),
                     in1=rsb[gi][:].rearrange("p (h w) -> p h w", w=32),
                     op=ALU.mult,
                 )
@@ -375,14 +385,28 @@ def tile_window_attention_t_kernel(tc, kv, q, mask, out):
                     in_=oa[(pr, cc)][:, h0:h1, :, :].rearrange("c h v w -> c (h v w)"),
                 )
 
-        vpe_at = {6: 0}
-        vq_at = {8: 0}
-        for inst in range(1, 8):
-            vpe_at[8 * inst + 4] = inst
-            vq_at[8 * inst + 6] = inst
+        def grp_at(s, d):
+            return by_last.get(s - d)
+
+        def half_at(s, d, cc):
+            gi = by_last.get(s - d[cc])
+            if gi is not None and groups[gi][0] >= 60:
+                gi = None
+            if gi is None:
+                gl = by_last.get(s - d[0])
+                if gl is not None and groups[gl][0] >= 60:
+                    gi = gl
+            return gi
+
+        vt_at = {}
+        vq_at = {}
+        for inst in range(8):
+            for cc in range(2):
+                vt_at[(max(8 * inst + D_VT[cc], 6), cc)] = inst
+            vq_at[max(8 * inst + D_QV, 8)] = inst
 
         load_pair(0)
-        for s in range(NT + T_LAG + 8):
+        for s in range(NT + T_LAG + 12):
             if s % 16 == 0 and s // 16 + 1 < 4:
                 load_pair(s // 16 + 1)
             j = s - T_LAG
@@ -392,38 +416,50 @@ def tile_window_attention_t_kernel(tc, kv, q, mask, out):
                 transposes(j, 0)
             if s < NT:
                 scores(s, 1)
-            if j - 3 in by_last:
-                mx(by_last[j - 3])
+            for cc in range(2):
+                if half_at(s, D_MX, cc) is not None:
+                    mx(half_at(s, D_MX, cc), cc)
             if 0 <= j < NT:
                 transposes(j, 1)
                 evac_tile(j)
-            if s in vpe_at:
-                vpath_pe(vpe_at[s])
-            if j - 1 in by_last:
-                spread_r(by_last[j - 1])
-            if 0 <= s - 2 < NT:
+            for cc in range(2):
+                if (s, cc) in vt_at:
+                    vpath_pe(vt_at[(s, cc)], cc)
+            if grp_at(s, D_RS) is not None:
+                spread_r(grp_at(s, D_RS))
+            if s < NT and on_ar(s):
+                for nh in range(2):
+                    ar_copy(s, nh)
+                for nh in range(2):
+                    ar_add(s, nh)
+            if 0 <= s - 2 < NT and not on_ar(s - 2):
                 exp_tile(s - 2)
-            if j - 3 in by_last and on_gp(by_last[j - 3]):
-                o_out(by_last[j - 3], 0)
-                o_out(by_last[j - 3], 1)
-            if s < NT:
+            for cc in range(2):
+                gi = half_at(s, D_O, cc)
+                if gi is not None and on_gp(gi):
+                    o_out(gi, cc)
+            if s < NT and not on_ar(s):
                 leave_psum(s, 0)
-            if 0 <= s - 1 < NT:
+            late = 0 <= s - 2 < NT and on_ar(s - 2)
+            if late:
+                row_min(s - 2)
+                exp_tile(s - 2)
+            if 0 <= s - 1 < NT and not on_ar(s - 1) and not late:
                 row_min(s - 1)
-            if s < NT:
+            if s < NT and not on_ar(s):
                 leave_psum(s, 1)
+            if late:
+                row_min(s - 1)
             if s in vq_at:
                 vpath_q(vq_at[s])
-            if s - 4 in by_last:
-                recip(by_last[s - 4])
-            if j - 1 in by_last:
-                quant_e(by_last[j - 1])
-            if j - 3 in by_last:
-                gi = by_last[j - 3]
-                norm_store(gi, 0)
-                if groups[gi][0] >= 60 or on_gp(gi):
-                    norm_store(gi, 1)
-            if j - 4 in by_last and groups[by_last[j - 4]][0] < 60 and not on_gp(by_last[j - 4]):
-                norm_store(by_last[j - 4], 1)
-            if 8 <= s % 16 < 12 and s // 16 + 1 < 4:
-                scale_q(s // 16 + 1, (s % 16 - 8) % 2, (s % 16 - 8) // 2, 0, 32)
+            if grp_at(s, D_RC) is not None:
+                recip(grp_at(s, D_RC))
+            if grp_at(s, D_QE) is not None:
+                quant_e(grp_at(s, D_QE))
+            for cc in range(2):
+                gi = half_at(s, D_M, cc)
+                if gi is not None:
+                    norm_store(gi, cc)
+            if s % 16 in D_SQ and s // 16 + 1 < 4:
+                k = D_SQ.index(s % 16)
+                scale_q(s // 16 + 1, k % 2, k // 2, 0, 32)

@@ -32,8 +32,11 @@ D_O = (8, 9)
 D_M = (8, 9)
 D_VT = (0, 4)
 D_QV = 6
-D_SQ = (8, 9, 10, 11)
+D_SQ = (7, 11, 15, 19)
 T_BUFS = 2
+PS_PERM = False
+HEAD = 0
+O_FIRST = True
 
 
 def tile_window_attention_t_kernel(tc, kv, q, mask, out):
@@ -141,7 +144,57 @@ def tile_window_attention_t_kernel(tc, kv, q, mask, out):
                 for v in range(2):
                     qs[(pr, cc, v)] = inp.tile([P, NKEY], BF16, name="qs%d%d" % (cc, v), tag="qs%d%d" % (cc, v))
                     vd[(pr, cc, v)] = inp.tile([P, NKEY], BF16, name="vd%d%d" % (cc, v), tag="vd%d%d" % (cc, v))
-            if pr == 0:
+            if pr == 0 and HEAD == 1:
+                for cc in range(2):
+                    load_q(pr, cc, 0, 8)
+                    scale_q(pr, cc, 0, 0, 8)
+                for cc in range(2):
+                    load_k(pr, cc, 0, 16)
+                load_mask(0, 0, 1)
+                for cc in range(2):
+                    load_k(pr, cc, 16, 32)
+                load_mask(0, 1, 1)
+                for cc in range(2):
+                    load_q(pr, cc, 8, 32)
+                    scale_q(pr, cc, 0, 8, 32)
+                load_mask(0, 2, 2)
+                load_mask(0, 4, 4)
+                for cc in range(2):
+                    load_v(pr, cc, 0)
+                for cc in range(2):
+                    scale_q(pr, cc, 1, 0, 32)
+                load_mask(1, 0, 4)
+                for cc in range(2):
+                    load_v(pr, cc, 1)
+                load_mask(1, 4, 4)
+            elif pr == 0 and HEAD == 2:
+                for cc in range(2):
+                    load_q(pr, cc, 0, 4)
+                    scale_q(pr, cc, 0, 0, 4)
+                for cc in range(2):
+                    load_k(pr, cc, 0, 16)
+                load_mask(0, 0, 1)
+                for cc in range(2):
+                    load_k(pr, cc, 16, 32)
+                for cc in range(2):
+                    load_q(pr, cc, 4, 32)
+                for qt in range(1, 4):
+                    for cc in range(2):
+                        scale_q(pr, cc, 0, 4 * qt, 4 * qt + 4)
+                for cc in range(2):
+                    scale_q(pr, cc, 0, 16, 32)
+                load_mask(0, 1, 1)
+                load_mask(0, 2, 2)
+                load_mask(0, 4, 4)
+                for cc in range(2):
+                    load_v(pr, cc, 0)
+                for cc in range(2):
+                    scale_q(pr, cc, 1, 0, 32)
+                load_mask(1, 0, 4)
+                for cc in range(2):
+                    load_v(pr, cc, 1)
+                load_mask(1, 4, 4)
+            elif pr == 0:
                 for cc in range(2):
                     load_q(pr, cc, 0, 4)
                     scale_q(pr, cc, 0, 0, 4)
@@ -192,6 +245,9 @@ def tile_window_attention_t_kernel(tc, kv, q, mask, out):
         def flat(ap):
             return ap.rearrange("q (u p e) -> q u p e", u=2, e=2)
 
+        def from_psum(ap):
+            return flat(ap) if PS_PERM else perm(ap)
+
         def half(nh):
             return slice(nh * 512, (nh + 1) * 512)
 
@@ -202,14 +258,22 @@ def tile_window_attention_t_kernel(tc, kv, q, mask, out):
             for cc in range(2):
                 kview = kraw[(pr, cc)][:].rearrange("c (h v w) -> c h v w", v=2, w=32)
                 nc.tensor.matmul(
-                    out=s_nh[:].rearrange("p (h w) -> p h w", w=32),
+                    out=(s_nh[:].rearrange("q (u h a e) -> q h a u e", u=2, h=16, e=2) if PS_PERM
+                         else s_nh[:].rearrange("p (h w) -> p h w", w=32)),
                     lhsT=qs[(pr, cc, v)][:, qt * P:(qt + 1) * P],
-                    rhs=kview[:, nh * 16:(nh + 1) * 16, v, :],
+                    rhs=(kview[:, nh * 16:(nh + 1) * 16, v, :].rearrange("c h (a u e) -> c h a u e", u=2, e=2) if PS_PERM
+                         else kview[:, nh * 16:(nh + 1) * 16, v, :]),
                     start=(cc == 0),
                     stop=(cc == 1 and not on_pe(i)),
                 )
             if on_pe(i):
-                nc.tensor.matmul(out=s_nh[:], lhsT=identm[:], rhs=mask_sb[v][:, qt, half(nh)], start=False, stop=True)
+                nc.tensor.matmul(
+                    out=(s_nh[:].rearrange("q (u m e) -> q m u e", u=2, e=2) if PS_PERM else s_nh[:]),
+                    lhsT=identm[:],
+                    rhs=(mask_sb[v][:, qt, half(nh)].rearrange("q (m u e) -> q m u e", u=2, e=2) if PS_PERM
+                         else mask_sb[v][:, qt, half(nh)]),
+                    start=False, stop=True,
+                )
 
         def transposes(i, part):
             if part == 0:
@@ -227,19 +291,19 @@ def tile_window_attention_t_kernel(tc, kv, q, mask, out):
             u = ut[i]
             if on_pe(i):
                 nc.vector.tensor_scalar(
-                    out=flat(u[:, half(nh)]), in0=perm(st[(i, nh)][:]), scalar1=1.0, scalar2=None,
+                    out=flat(u[:, half(nh)]), in0=from_psum(st[(i, nh)][:]), scalar1=1.0, scalar2=None,
                     op0=ALU.mult, op1=ALU.min, accum_out=nm2t[i][:, nh:nh + 1],
                 )
             else:
                 nc.vector.tensor_tensor(
-                    out=flat(u[:, half(nh)]), in0=perm(st[(i, nh)][:]), in1=perm(mask_sb[v][:, qt, half(nh)]),
+                    out=flat(u[:, half(nh)]), in0=from_psum(st[(i, nh)][:]), in1=perm(mask_sb[v][:, qt, half(nh)]),
                     op=ALU.subtract,
                 )
 
         def ar_copy(i, nh):
             if nh == 0:
                 tqt[i] = work.tile([P, NKEY], F32, name="tq", tag="tq", bufs=2)
-            nc.scalar.copy(out=flat(tqt[i][:, half(nh)]), in_=perm(st[(i, nh)][:]))
+            nc.scalar.copy(out=flat(tqt[i][:, half(nh)]), in_=from_psum(st[(i, nh)][:]))
 
         def ar_add(i, nh):
             pr, v, qt = where(i)
@@ -405,6 +469,11 @@ def tile_window_attention_t_kernel(tc, kv, q, mask, out):
                 vt_at[(max(8 * inst + D_VT[cc], 6), cc)] = inst
             vq_at[max(8 * inst + D_QV, 8)] = inst
 
+        sq_at = {}
+        for pr in range(1, 4):
+            for k in range(4):
+                sq_at[16 * (pr - 1) + D_SQ[k]] = (pr, k % 2, k // 2)
+
         load_pair(0)
         for s in range(NT + T_LAG + 12):
             if s % 16 == 0 and s // 16 + 1 < 4:
@@ -432,19 +501,24 @@ def tile_window_attention_t_kernel(tc, kv, q, mask, out):
                     ar_copy(s, nh)
                 for nh in range(2):
                     ar_add(s, nh)
-            if 0 <= s - 2 < NT and not on_ar(s - 2):
+            if 0 <= s - 2 < NT and not on_ar(s - 2) and not O_FIRST:
                 exp_tile(s - 2)
             for cc in range(2):
                 gi = half_at(s, D_O, cc)
                 if gi is not None and on_gp(gi):
                     o_out(gi, cc)
+            if 0 <= s - 2 < NT and not on_ar(s - 2) and O_FIRST:
+                exp_tile(s - 2)
+            first = HEAD >= 1 and s == 1
+            if first:
+                row_min(0)
             if s < NT and not on_ar(s):
                 leave_psum(s, 0)
             late = 0 <= s - 2 < NT and on_ar(s - 2)
             if late:
                 row_min(s - 2)
                 exp_tile(s - 2)
-            if 0 <= s - 1 < NT and not on_ar(s - 1) and not late:
+            if 0 <= s - 1 < NT and not on_ar(s - 1) and not late and not first:
                 row_min(s - 1)
             if s < NT and not on_ar(s):
                 leave_psum(s, 1)
@@ -460,6 +534,5 @@ def tile_window_attention_t_kernel(tc, kv, q, mask, out):
                 gi = half_at(s, D_M, cc)
                 if gi is not None:
                     norm_store(gi, cc)
-            if s % 16 in D_SQ and s // 16 + 1 < 4:
-                k = D_SQ.index(s % 16)
-                scale_q(s // 16 + 1, k % 2, k // 2, 0, 32)
+            if s in sq_at:
+                scale_q(sq_at[s][0], sq_at[s][1], sq_at[s][2], 0, 32)

@@ -19,7 +19,7 @@ FLOPS = 2 * 2 * 8 * 1024 * 1024 * 256
 
 T_LAG = 5
 E_BUFS = 5
-U_BUFS = 4
+U_BUFS = 7
 PE_MASK = (2, 7, 12)
 AR_SET = ()
 LAST_SPLIT = (2, 1, 1)
@@ -37,6 +37,7 @@ T_BUFS = 2
 PS_PERM = False
 HEAD = 0
 O_FIRST = True
+TR_MODE = 0
 
 
 def tile_window_attention_t_kernel(tc, kv, q, mask, out):
@@ -483,19 +484,29 @@ def tile_window_attention_t_kernel(tc, kv, q, mask, out):
                 scores(s, 0)
             if 0 <= j < NT:
                 transposes(j, 0)
+                if TR_MODE >= 1:
+                    transposes(j, 1)
+                    evac_tile(j)
+            if TR_MODE == 2:
+                for cc in range(2):
+                    if (s, cc) in vt_at:
+                        vpath_pe(vt_at[(s, cc)], cc)
+                if grp_at(s, D_RS) is not None:
+                    spread_r(grp_at(s, D_RS))
             if s < NT:
                 scores(s, 1)
             for cc in range(2):
                 if half_at(s, D_MX, cc) is not None:
                     mx(half_at(s, D_MX, cc), cc)
-            if 0 <= j < NT:
+            if 0 <= j < NT and TR_MODE == 0:
                 transposes(j, 1)
                 evac_tile(j)
-            for cc in range(2):
-                if (s, cc) in vt_at:
-                    vpath_pe(vt_at[(s, cc)], cc)
-            if grp_at(s, D_RS) is not None:
-                spread_r(grp_at(s, D_RS))
+            if TR_MODE < 2:
+                for cc in range(2):
+                    if (s, cc) in vt_at:
+                        vpath_pe(vt_at[(s, cc)], cc)
+                if grp_at(s, D_RS) is not None:
+                    spread_r(grp_at(s, D_RS))
             if s < NT and on_ar(s):
                 for nh in range(2):
                     ar_copy(s, nh)

@@ -31,13 +31,14 @@ D_MX = (8, 9)
 D_O = (8, 9)
 D_M = (8, 9)
 D_VT = (0, 4)
-D_QV = 6
+D_QV = 5
 D_SQ = (7, 11, 15, 19)
 T_BUFS = 2
 PS_PERM = False
 HEAD = 0
 O_FIRST = True
 TR_MODE = 0
+MX_EARLY = True
 
 
 def tile_window_attention_t_kernel(tc, kv, q, mask, out):
@@ -482,6 +483,13 @@ def tile_window_attention_t_kernel(tc, kv, q, mask, out):
             j = s - T_LAG
             if s < NT:
                 scores(s, 0)
+            if MX_EARLY:
+                for cc in range(2):
+                    gi = half_at(s, D_MX, cc)
+                    if gi is not None:
+                        mx(gi, cc)
+                        if on_gp(gi):
+                            o_out(gi, cc)
             if 0 <= j < NT:
                 transposes(j, 0)
                 if TR_MODE >= 1:
@@ -496,7 +504,7 @@ def tile_window_attention_t_kernel(tc, kv, q, mask, out):
             if s < NT:
                 scores(s, 1)
             for cc in range(2):
-                if half_at(s, D_MX, cc) is not None:
+                if half_at(s, D_MX, cc) is not None and not MX_EARLY:
                     mx(half_at(s, D_MX, cc), cc)
             if 0 <= j < NT and TR_MODE == 0:
                 transposes(j, 1)
@@ -516,7 +524,7 @@ def tile_window_attention_t_kernel(tc, kv, q, mask, out):
                 exp_tile(s - 2)
             for cc in range(2):
                 gi = half_at(s, D_O, cc)
-                if gi is not None and on_gp(gi):
+                if gi is not None and on_gp(gi) and not MX_EARLY:
                     o_out(gi, cc)
             if 0 <= s - 2 < NT and not on_ar(s - 2) and O_FIRST:
                 exp_tile(s - 2)

@@ -25,8 +25,8 @@ AR_SET = ()
 LAST_SPLIT = (2, 1, 1)
 GP_UNTIL = 56
 D_QE = 6
-D_RC = 4
-D_RS = 6
+D_RC = 6
+D_RS = 7
 D_MX = (8, 9)
 D_O = (8, 9)
 D_M = (8, 9)
@@ -39,6 +39,14 @@ HEAD = 0
 O_FIRST = True
 TR_MODE = 0
 MX_EARLY = True
+PE_SWAP = ()
+PE_CHAIN = True
+TAIL = 0
+Q_BUFS = 2
+XV_FROM = 99
+XV_SET = ()
+TAIL_ORDER = 0
+RBV_FROM = 99
 
 
 def tile_window_attention_t_kernel(tc, kv, q, mask, out):
@@ -98,6 +106,7 @@ def tile_window_attention_t_kernel(tc, kv, q, mask, out):
         ot = {}
         osb = {}
         tqt = {}
+        otl = {}
 
         def chan0(pr, cc):
             return (pr % 2) * 256 + cc * P
@@ -236,6 +245,10 @@ def tile_window_attention_t_kernel(tc, kv, q, mask, out):
             return inst // 2, inst % 2, i % 8
 
         def on_pe(i):
+            if PE_SWAP and i == PE_SWAP[0]:
+                return False
+            if PE_SWAP and i == PE_SWAP[1]:
+                return True
             return i % 16 in PE_MASK
 
         def on_ar(i):
@@ -278,7 +291,11 @@ def tile_window_attention_t_kernel(tc, kv, q, mask, out):
                 )
 
         def transposes(i, part):
-            if part == 0:
+            if part == 0 and TAIL == 2 and i >= 61:
+                xtt[i] = ps_s.tile([P, 4, P], F32, name="xs%d" % i, tag="s%d" % ((i - 61) % 2))
+            elif part == 0 and TAIL == 1 and i >= 62:
+                xtt[i] = ps_s.tile([P, 4, P], F32, name="xs%d" % (i - 62), tag="s%d" % (i - 62))
+            elif part == 0:
                 xtt[i] = ps_t.tile([P, 4, P], F32, name="xt", tag="t")
             ewords = et[i][:].bitcast(F32)
             for kb in range(2 * part, 2 * part + 2):
@@ -291,7 +308,13 @@ def tile_window_attention_t_kernel(tc, kv, q, mask, out):
                 if on_pe(i):
                     nm2t[i] = work.tile([P, 2], F32, name="nm2", tag="nm2", bufs=2)
             u = ut[i]
-            if on_pe(i):
+            if on_pe(i) and PE_CHAIN and nh == 1:
+                nmt[i] = work.tile([P, 1], F32, name="nm", tag="nm", bufs=6)
+                nc.vector.tensor_scalar(
+                    out=flat(u[:, half(nh)]), in0=from_psum(st[(i, nh)][:]), scalar1=1.0, scalar2=nm2t[i][:, 0:1],
+                    op0=ALU.mult, op1=ALU.min, accum_out=nmt[i][:],
+                )
+            elif on_pe(i):
                 nc.vector.tensor_scalar(
                     out=flat(u[:, half(nh)]), in0=from_psum(st[(i, nh)][:]), scalar1=1.0, scalar2=None,
                     op0=ALU.mult, op1=ALU.min, accum_out=nm2t[i][:, nh:nh + 1],
@@ -317,6 +340,8 @@ def tile_window_attention_t_kernel(tc, kv, q, mask, out):
             )
 
         def row_min(i):
+            if on_pe(i) and PE_CHAIN:
+                return
             nm = work.tile([P, 1], F32, name="nm", tag="nm", bufs=6)
             nmt[i] = nm
             if on_pe(i):
@@ -341,12 +366,18 @@ def tile_window_attention_t_kernel(tc, kv, q, mask, out):
             g0, gn = groups[gi]
             jj = i - g0
             if jj == 0:
-                grp[gi] = work.tile([P, 2, gn * P, 4], BF16, name="grp", tag="grp", bufs=2, align_bytes=64)
+                grp[gi] = work.tile([P, 2, gn * P, 4], BF16, name="grp", tag="grp", bufs=Q_BUFS, align_bytes=64)
             gw = grp[gi][:].rearrange("p g n t -> p (g n t)").bitcast(F32).rearrange("p (g n u) -> p g n u", g=2, u=2)
-            nc.scalar.copy(
-                out=gw[:, :, jj * P:(jj + 1) * P, :],
-                in_=xtt[i][:].rearrange("p (g u) n -> p g n u", u=2),
-            )
+            if i >= XV_FROM or i in XV_SET:
+                nc.vector.tensor_copy(
+                    out=gw[:, :, jj * P:(jj + 1) * P, :],
+                    in_=xtt[i][:].rearrange("p (g u) n -> p g n u", u=2),
+                )
+            else:
+                nc.scalar.copy(
+                    out=gw[:, :, jj * P:(jj + 1) * P, :],
+                    in_=xtt[i][:].rearrange("p (g u) n -> p g n u", u=2),
+                )
 
         def vpath_pe(inst, cc):
             pr, v = inst // 2, inst % 2
@@ -379,8 +410,8 @@ def tile_window_attention_t_kernel(tc, kv, q, mask, out):
 
         def quant_e(gi):
             g0, gn = groups[gi]
-            ecode[gi] = work.tile([P, 2 * gn * P], U32, name="ecode", tag="ecode", bufs=2, align_bytes=64)
-            escale[gi] = work.tile([P, 2 * gn * P], U8, name="escale", tag="escale", bufs=2, align_bytes=64)
+            ecode[gi] = work.tile([P, 2 * gn * P], U32, name="ecode", tag="ecode", bufs=Q_BUFS, align_bytes=64)
+            escale[gi] = work.tile([P, 2 * gn * P], U8, name="escale", tag="escale", bufs=Q_BUFS, align_bytes=64)
             nc.vector.quantize_mx(
                 out=ecode[gi][:].bitcast(FP8X4),
                 scales=escale[gi][:],
@@ -397,17 +428,29 @@ def tile_window_attention_t_kernel(tc, kv, q, mask, out):
                     identity=ident_f[:],
                 )
             rsb[gi] = work.tile([P, gn * P], F32, name="rsb", tag="rsb", bufs=3)
-            nc.scalar.copy(out=rsb[gi][:], in_=rp[:])
+            if gi >= RBV_FROM:
+                nc.vector.tensor_copy(out=rsb[gi][:], in_=rp[:])
+            else:
+                nc.scalar.copy(out=rsb[gi][:], in_=rp[:])
 
         def mx(gi, cc):
             g0, gn = groups[gi]
             inst = g0 // 8
             w = gn * P
-            ot[(gi, cc)] = ps_o.tile([P, w], F32, name="o%d" % cc, tag="o%d" % cc)
+            if TAIL == 2 and g0 >= 60:
+                if cc == 0:
+                    otl[gi] = ps_s.tile([P, 2, w], F32, name="ol%d" % gi, tag="s%d" % ((gi - 14) % 2))
+                ot[(gi, cc)] = otl[gi][:, cc, :]
+            elif TAIL == 1 and gi == len(groups) - 2:
+                o_t = ps_s.tile([P, w], F32, name="os%d" % cc, tag="s%d" % cc)
+                ot[(gi, cc)] = o_t[:]
+            else:
+                o_t = ps_o.tile([P, w], F32, name="o%d" % cc, tag="o%d" % cc)
+                ot[(gi, cc)] = o_t[:]
             for g in range(2):
                 w0 = g * 256 + cc * P
                 nc.tensor.matmul_mx(
-                    out=ot[(gi, cc)][:],
+                    out=ot[(gi, cc)],
                     lhsT=vcode[inst][:, w0:w0 + P].bitcast(FP8X4),
                     lhsT_scale=vscale[inst][:, w0:w0 + P],
                     rhs=ecode[gi][:, g * w:(g + 1) * w].bitcast(FP8X4),
@@ -422,7 +465,7 @@ def tile_window_attention_t_kernel(tc, kv, q, mask, out):
         def o_out(gi, cc):
             g0, gn = groups[gi]
             osb[(gi, cc)] = work.tile([P, gn * P], F32, name="osb%d" % cc, tag="osb%d" % cc, bufs=2)
-            nc.scalar.copy(out=osb[(gi, cc)][:], in_=ot[(gi, cc)][:])
+            nc.scalar.copy(out=osb[(gi, cc)][:], in_=ot[(gi, cc)])
 
         def norm_store(gi, cc):
             g0, gn = groups[gi]
@@ -440,7 +483,7 @@ def tile_window_attention_t_kernel(tc, kv, q, mask, out):
             else:
                 nc.vector.tensor_tensor(
                     out=oa[(pr, cc)][:, h0:h1, v, :],
-                    in0=ot[(gi, cc)][:].rearrange("p (h w) -> p h w", w=32),
+                    in0=ot[(gi, cc)].rearrange("p (h w) -> p h w", w=32),
                     in1=rsb[gi][:].rearrange("p (h w) -> p h w", w=32),
                     op=ALU.mult,
                 )
@@ -476,11 +519,95 @@ def tile_window_attention_t_kernel(tc, kv, q, mask, out):
             for k in range(4):
                 sq_at[16 * (pr - 1) + D_SQ[k]] = (pr, k % 2, k // 2)
 
+        def tr_x(i):
+            transposes(i, 0)
+            transposes(i, 1)
+            evac_tile(i)
+
+        def tail_a():
+            exp_tile(62)
+            row_min(63)
+            tr_x(59)
+            exp_tile(63)
+            tr_x(60)
+            tr_x(61)
+            spread_r(14)
+            mx(13, 1)
+            o_out(13, 1)
+            norm_store(13, 1)
+            quant_e(14)
+            recip(15)
+            tr_x(62)
+            tr_x(63)
+            mx(14, 0)
+            mx(14, 1)
+            quant_e(15)
+            recip(16)
+            recip(17)
+            spread_r(15)
+            norm_store(14, 0)
+            norm_store(14, 1)
+            quant_e(16)
+            quant_e(17)
+            spread_r(16)
+            spread_r(17)
+            for gi in (15, 16, 17):
+                for cc in range(2):
+                    mx(gi, cc)
+            for gi in (15, 16, 17):
+                for cc in range(2):
+                    norm_store(gi, cc)
+
+        def tail():
+            if TAIL_ORDER == 0:
+                tail_a()
+            else:
+                tail_b()
+
+        def tail_b():
+            exp_tile(62)
+            row_min(63)
+            tr_x(59)
+            exp_tile(63)
+            quant_e(14)
+            tr_x(60)
+            tr_x(61)
+            spread_r(14)
+            mx(13, 1)
+            o_out(13, 1)
+            norm_store(13, 1)
+            recip(15)
+            tr_x(62)
+            tr_x(63)
+            mx(14, 0)
+            mx(14, 1)
+            quant_e(15)
+            recip(16)
+            recip(17)
+            spread_r(15)
+            norm_store(14, 0)
+            norm_store(14, 1)
+            quant_e(16)
+            quant_e(17)
+            for cc in range(2):
+                mx(15, cc)
+            spread_r(16)
+            spread_r(17)
+            for gi in (16, 17):
+                for cc in range(2):
+                    mx(gi, cc)
+            for gi in (15, 16, 17):
+                for cc in range(2):
+                    norm_store(gi, cc)
+
         load_pair(0)
-        for s in range(NT + T_LAG + 12):
+        for s in range(NT if TAIL == 2 else NT + T_LAG + 12):
             if s % 16 == 0 and s // 16 + 1 < 4:
                 load_pair(s // 16 + 1)
             j = s - T_LAG
+            e_first = TAIL >= 1 and s >= NT
+            if e_first and 0 <= s - 2 < NT:
+                exp_tile(s - 2)
             if s < NT:
                 scores(s, 0)
             if MX_EARLY:
@@ -520,13 +647,13 @@ def tile_window_attention_t_kernel(tc, kv, q, mask, out):
                     ar_copy(s, nh)
                 for nh in range(2):
                     ar_add(s, nh)
-            if 0 <= s - 2 < NT and not on_ar(s - 2) and not O_FIRST:
+            if 0 <= s - 2 < NT and not on_ar(s - 2) and not O_FIRST and not e_first:
                 exp_tile(s - 2)
             for cc in range(2):
                 gi = half_at(s, D_O, cc)
                 if gi is not None and on_gp(gi) and not MX_EARLY:
                     o_out(gi, cc)
-            if 0 <= s - 2 < NT and not on_ar(s - 2) and O_FIRST:
+            if 0 <= s - 2 < NT and not on_ar(s - 2) and O_FIRST and not e_first:
                 exp_tile(s - 2)
             first = HEAD >= 1 and s == 1
             if first:
@@ -555,3 +682,5 @@ def tile_window_attention_t_kernel(tc, kv, q, mask, out):
                     norm_store(gi, cc)
             if s in sq_at:
                 scale_q(sq_at[s][0], sq_at[s][1], sq_at[s][2], 0, 32)
+        if TAIL == 2:
+            tail()

@@ -21,32 +21,27 @@ T_LAG = 5
 E_BUFS = 5
 U_BUFS = 7
 PE_MASK = (2, 7, 12)
-AR_SET = ()
-LAST_SPLIT = (2, 1, 1)
-GP_UNTIL = 56
+MT_SET = (4, 9, 14)
+MT_LEAD = 2
+MT_FROM = 5
+MT_V = ()
+LAST_SPLIT = (2, 2)
+GP_UNTIL = 52
+DMA_INSTS = 7
 D_QE = 6
 D_RC = 6
 D_RS = 7
 D_MX = (8, 9)
-D_O = (8, 9)
 D_M = (8, 9)
+D_LAST = (3, 4, (7, 8), (99, 99))
+D_MD5 = ((12, 12), (13, 14))
+V_EVAC = (59, 60)
+TAIL_S = (60, 61, 62, 63)
+D_RD = 7
+D_MD = ((12, 13), (16, 17))
 D_VT = (0, 4)
 D_QV = 5
 D_SQ = (7, 11, 15, 19)
-T_BUFS = 2
-PS_PERM = False
-HEAD = 0
-O_FIRST = True
-TR_MODE = 0
-MX_EARLY = True
-PE_SWAP = ()
-PE_CHAIN = True
-TAIL = 0
-Q_BUFS = 2
-XV_FROM = 99
-XV_SET = ()
-TAIL_ORDER = 0
-RBV_FROM = 99
 
 
 def tile_window_attention_t_kernel(tc, kv, q, mask, out):
@@ -57,7 +52,7 @@ def tile_window_attention_t_kernel(tc, kv, q, mask, out):
         inp = ctx.enter_context(tc.tile_pool(name="inp", bufs=2))
         work = ctx.enter_context(tc.tile_pool(name="work", bufs=2))
         ps_s = ctx.enter_context(tc.psum_pool(name="ps_s", bufs=2))
-        ps_t = ctx.enter_context(tc.psum_pool(name="ps_t", bufs=T_BUFS))
+        ps_t = ctx.enter_context(tc.psum_pool(name="ps_t", bufs=2))
         ps_o = ctx.enter_context(tc.psum_pool(name="ps_o", bufs=1))
         ctx.enter_context(tc.manual_schedule())
 
@@ -69,6 +64,7 @@ def tile_window_attention_t_kernel(tc, kv, q, mask, out):
         nc.vector.tensor_scalar_mul(out=identm[:], in0=ident_bf[:], scalar1=-1.0)
 
         mask_sb = [maskp.tile([P, 8, NKEY], BF16, name="mask%d" % v) for v in range(2)]
+        rpad = [const.tile([P, P], F32, name="rpad%d" % k) for k in range(2)]
 
         groups = [(4 * h, 4) for h in range(15)]
         first = 60
@@ -101,12 +97,13 @@ def tile_window_attention_t_kernel(tc, kv, q, mask, out):
         rst = {}
         rt = {}
         rsb = {}
+        rpt = {}
+        rsi = {}
+        rbt = {}
         ecode = {}
         escale = {}
         ot = {}
-        osb = {}
-        tqt = {}
-        otl = {}
+        mt = {}
 
         def chan0(pr, cc):
             return (pr % 2) * 256 + cc * P
@@ -155,57 +152,7 @@ def tile_window_attention_t_kernel(tc, kv, q, mask, out):
                 for v in range(2):
                     qs[(pr, cc, v)] = inp.tile([P, NKEY], BF16, name="qs%d%d" % (cc, v), tag="qs%d%d" % (cc, v))
                     vd[(pr, cc, v)] = inp.tile([P, NKEY], BF16, name="vd%d%d" % (cc, v), tag="vd%d%d" % (cc, v))
-            if pr == 0 and HEAD == 1:
-                for cc in range(2):
-                    load_q(pr, cc, 0, 8)
-                    scale_q(pr, cc, 0, 0, 8)
-                for cc in range(2):
-                    load_k(pr, cc, 0, 16)
-                load_mask(0, 0, 1)
-                for cc in range(2):
-                    load_k(pr, cc, 16, 32)
-                load_mask(0, 1, 1)
-                for cc in range(2):
-                    load_q(pr, cc, 8, 32)
-                    scale_q(pr, cc, 0, 8, 32)
-                load_mask(0, 2, 2)
-                load_mask(0, 4, 4)
-                for cc in range(2):
-                    load_v(pr, cc, 0)
-                for cc in range(2):
-                    scale_q(pr, cc, 1, 0, 32)
-                load_mask(1, 0, 4)
-                for cc in range(2):
-                    load_v(pr, cc, 1)
-                load_mask(1, 4, 4)
-            elif pr == 0 and HEAD == 2:
-                for cc in range(2):
-                    load_q(pr, cc, 0, 4)
-                    scale_q(pr, cc, 0, 0, 4)
-                for cc in range(2):
-                    load_k(pr, cc, 0, 16)
-                load_mask(0, 0, 1)
-                for cc in range(2):
-                    load_k(pr, cc, 16, 32)
-                for cc in range(2):
-                    load_q(pr, cc, 4, 32)
-                for qt in range(1, 4):
-                    for cc in range(2):
-                        scale_q(pr, cc, 0, 4 * qt, 4 * qt + 4)
-                for cc in range(2):
-                    scale_q(pr, cc, 0, 16, 32)
-                load_mask(0, 1, 1)
-                load_mask(0, 2, 2)
-                load_mask(0, 4, 4)
-                for cc in range(2):
-                    load_v(pr, cc, 0)
-                for cc in range(2):
-                    scale_q(pr, cc, 1, 0, 32)
-                load_mask(1, 0, 4)
-                for cc in range(2):
-                    load_v(pr, cc, 1)
-                load_mask(1, 4, 4)
-            elif pr == 0:
+            if pr == 0:
                 for cc in range(2):
                     load_q(pr, cc, 0, 4)
                     scale_q(pr, cc, 0, 0, 4)
@@ -245,14 +192,13 @@ def tile_window_attention_t_kernel(tc, kv, q, mask, out):
             return inst // 2, inst % 2, i % 8
 
         def on_pe(i):
-            if PE_SWAP and i == PE_SWAP[0]:
-                return False
-            if PE_SWAP and i == PE_SWAP[1]:
-                return True
             return i % 16 in PE_MASK
 
-        def on_ar(i):
-            return i % 16 in AR_SET
+        def on_mt(i):
+            return i >= MT_FROM and i % 16 in MT_SET
+
+        def in_psum(i):
+            return on_pe(i) or on_mt(i)
 
         def perm(ap):
             return ap.rearrange("q (p u e) -> q u p e", u=2, e=2)
@@ -260,41 +206,36 @@ def tile_window_attention_t_kernel(tc, kv, q, mask, out):
         def flat(ap):
             return ap.rearrange("q (u p e) -> q u p e", u=2, e=2)
 
-        def from_psum(ap):
-            return flat(ap) if PS_PERM else perm(ap)
-
         def half(nh):
             return slice(nh * 512, (nh + 1) * 512)
 
-        def scores(i, nh):
+        def scores(i, nh, between=None):
             pr, v, qt = where(i)
             s_nh = ps_s.tile([P, 512], F32, name="s%d" % nh, tag="s%d" % nh)
             st[(i, nh)] = s_nh
             for cc in range(2):
+                if cc == 1 and between is not None:
+                    between()
                 kview = kraw[(pr, cc)][:].rearrange("c (h v w) -> c h v w", v=2, w=32)
                 nc.tensor.matmul(
-                    out=(s_nh[:].rearrange("q (u h a e) -> q h a u e", u=2, h=16, e=2) if PS_PERM
-                         else s_nh[:].rearrange("p (h w) -> p h w", w=32)),
+                    out=s_nh[:].rearrange("p (h w) -> p h w", w=32),
                     lhsT=qs[(pr, cc, v)][:, qt * P:(qt + 1) * P],
-                    rhs=(kview[:, nh * 16:(nh + 1) * 16, v, :].rearrange("c h (a u e) -> c h a u e", u=2, e=2) if PS_PERM
-                         else kview[:, nh * 16:(nh + 1) * 16, v, :]),
+                    rhs=kview[:, nh * 16:(nh + 1) * 16, v, :],
                     start=(cc == 0),
-                    stop=(cc == 1 and not on_pe(i)),
+                    stop=(cc == 1 and not in_psum(i)),
                 )
+            if on_mt(i):
+                for kb in range(4):
+                    nc.tensor.matmul(
+                        out=s_nh[:, kb * P:(kb + 1) * P], lhsT=mt[i % 16][:, 4 * nh + kb, :], rhs=ident_f[:],
+                        is_transpose=True, start=False, stop=(kb == 3),
+                    )
             if on_pe(i):
-                nc.tensor.matmul(
-                    out=(s_nh[:].rearrange("q (u m e) -> q m u e", u=2, e=2) if PS_PERM else s_nh[:]),
-                    lhsT=identm[:],
-                    rhs=(mask_sb[v][:, qt, half(nh)].rearrange("q (m u e) -> q m u e", u=2, e=2) if PS_PERM
-                         else mask_sb[v][:, qt, half(nh)]),
-                    start=False, stop=True,
-                )
+                nc.tensor.matmul(out=s_nh[:], lhsT=identm[:], rhs=mask_sb[v][:, qt, half(nh)], start=False, stop=True)
 
         def transposes(i, part):
-            if part == 0 and TAIL == 2 and i >= 61:
-                xtt[i] = ps_s.tile([P, 4, P], F32, name="xs%d" % i, tag="s%d" % ((i - 61) % 2))
-            elif part == 0 and TAIL == 1 and i >= 62:
-                xtt[i] = ps_s.tile([P, 4, P], F32, name="xs%d" % (i - 62), tag="s%d" % (i - 62))
+            if part == 0 and i in TAIL_S:
+                xtt[i] = ps_s.tile([P, 4, P], F32, name="xs%d" % (i % 2), tag="s%d" % (i % 2))
             elif part == 0:
                 xtt[i] = ps_t.tile([P, 4, P], F32, name="xt", tag="t")
             ewords = et[i][:].bitcast(F32)
@@ -305,79 +246,75 @@ def tile_window_attention_t_kernel(tc, kv, q, mask, out):
             pr, v, qt = where(i)
             if nh == 0:
                 ut[i] = work.tile([P, NKEY], F32, name="u", tag="u", bufs=U_BUFS)
-                if on_pe(i):
-                    nm2t[i] = work.tile([P, 2], F32, name="nm2", tag="nm2", bufs=2)
+                if in_psum(i):
+                    nm2t[i] = work.tile([P, 1], F32, name="nm2", tag="nm2", bufs=2)
             u = ut[i]
-            if on_pe(i) and PE_CHAIN and nh == 1:
+            if in_psum(i) and nh == 1:
                 nmt[i] = work.tile([P, 1], F32, name="nm", tag="nm", bufs=6)
                 nc.vector.tensor_scalar(
-                    out=flat(u[:, half(nh)]), in0=from_psum(st[(i, nh)][:]), scalar1=1.0, scalar2=nm2t[i][:, 0:1],
+                    out=flat(u[:, half(nh)]), in0=perm(st[(i, nh)][:]), scalar1=1.0, scalar2=nm2t[i][:],
                     op0=ALU.mult, op1=ALU.min, accum_out=nmt[i][:],
                 )
-            elif on_pe(i):
+            elif in_psum(i):
                 nc.vector.tensor_scalar(
-                    out=flat(u[:, half(nh)]), in0=from_psum(st[(i, nh)][:]), scalar1=1.0, scalar2=None,
-                    op0=ALU.mult, op1=ALU.min, accum_out=nm2t[i][:, nh:nh + 1],
+                    out=flat(u[:, half(nh)]), in0=perm(st[(i, nh)][:]), scalar1=1.0, scalar2=None,
+                    op0=ALU.mult, op1=ALU.min, accum_out=nm2t[i][:],
                 )
             else:
                 nc.vector.tensor_tensor(
-                    out=flat(u[:, half(nh)]), in0=from_psum(st[(i, nh)][:]), in1=perm(mask_sb[v][:, qt, half(nh)]),
+                    out=flat(u[:, half(nh)]), in0=perm(st[(i, nh)][:]), in1=perm(mask_sb[v][:, qt, half(nh)]),
                     op=ALU.subtract,
                 )
 
-        def ar_copy(i, nh):
-            if nh == 0:
-                tqt[i] = work.tile([P, NKEY], F32, name="tq", tag="tq", bufs=2)
-            nc.scalar.copy(out=flat(tqt[i][:, half(nh)]), in_=from_psum(st[(i, nh)][:]))
-
-        def ar_add(i, nh):
-            pr, v, qt = where(i)
-            if nh == 0:
-                ut[i] = work.tile([P, NKEY], F32, name="ua", tag="ua", bufs=2)
-            nc.gpsimd.tensor_tensor(
-                out=flat(ut[i][:, half(nh)]), in0=flat(tqt[i][:, half(nh)]), in1=perm(mask_sb[v][:, qt, half(nh)]),
-                op=ALU.subtract,
-            )
+        def build_mt(k):
+            v, qt = k // 8, k % 8
+            pt = ps_t.tile([P, 8, P], BF16, name="pm", tag="t")
+            for kb in range(8):
+                nc.tensor.transpose(out=pt[:, kb, :], in_=mask_sb[v][:, qt, kb * P:(kb + 1) * P], identity=ident_bf[:])
+            mt[k] = maskp.tile([P, 8, P], F32, name="mt%d" % k)
+            if k in MT_V:
+                nc.vector.tensor_scalar_mul(out=mt[k][:], in0=pt[:], scalar1=-1.0)
+            else:
+                nc.scalar.activation(out=mt[k][:], in_=pt[:], func=ACT.Copy, scale=-1.0)
 
         def row_min(i):
-            if on_pe(i) and PE_CHAIN:
+            if in_psum(i):
                 return
             nm = work.tile([P, 1], F32, name="nm", tag="nm", bufs=6)
             nmt[i] = nm
-            if on_pe(i):
-                nc.vector.tensor_tensor(out=nm[:], in0=nm2t[i][:, 0:1], in1=nm2t[i][:, 1:2], op=ALU.min)
-            else:
-                nc.vector.tensor_reduce(out=nm[:], in_=ut[i][:], axis=AX.X, op=ALU.min)
+            nc.vector.tensor_reduce(out=nm[:], in_=ut[i][:], axis=AX.X, op=ALU.min)
+
+        def by_dma(i):
+            return i // 8 < DMA_INSTS
 
         def exp_tile(i):
             gi = group_of[i]
             g0, gn = groups[gi]
-            if i == g0:
-                rst[gi] = work.tile([P, 4], F32, name="rs", tag="rs", bufs=4)
+            if by_dma(i):
+                if i % 8 == 0:
+                    rsi[i // 8] = work.tile([P, 8], F32, name="rsi", tag="rsi", bufs=2)
+                col = rsi[i // 8][:, i % 8:i % 8 + 1]
+            else:
+                if i == g0:
+                    rst[gi] = work.tile([P, 4], F32, name="rs", tag="rs", bufs=4)
+                col = rst[gi][:, i - g0:i - g0 + 1]
             e = work.tile([P, NKEY], BF16, name="e", tag="e", bufs=E_BUFS)
             et[i] = e
-            nc.scalar.activation(
-                out=e[:], in_=ut[i][:], func=ACT.Exp, bias=nmt[i][:], scale=-1.0,
-                accum_out=rst[gi][:, i - g0:i - g0 + 1],
-            )
+            nc.scalar.activation(out=e[:], in_=ut[i][:], func=ACT.Exp, bias=nmt[i][:], scale=-1.0, accum_out=col)
 
         def evac_tile(i):
             gi = group_of[i]
             g0, gn = groups[gi]
             jj = i - g0
             if jj == 0:
-                grp[gi] = work.tile([P, 2, gn * P, 4], BF16, name="grp", tag="grp", bufs=Q_BUFS, align_bytes=64)
+                grp[gi] = work.tile([P, 2, gn * P, 4], BF16, name="grp", tag="grp", bufs=2, align_bytes=64)
             gw = grp[gi][:].rearrange("p g n t -> p (g n t)").bitcast(F32).rearrange("p (g n u) -> p g n u", g=2, u=2)
-            if i >= XV_FROM or i in XV_SET:
-                nc.vector.tensor_copy(
-                    out=gw[:, :, jj * P:(jj + 1) * P, :],
-                    in_=xtt[i][:].rearrange("p (g u) n -> p g n u", u=2),
-                )
+            ew = gw[:, :, jj * P:(jj + 1) * P, :]
+            xw = xtt[i][:].rearrange("p (g u) n -> p g n u", u=2)
+            if i in V_EVAC:
+                nc.vector.tensor_copy(out=ew, in_=xw)
             else:
-                nc.scalar.copy(
-                    out=gw[:, :, jj * P:(jj + 1) * P, :],
-                    in_=xtt[i][:].rearrange("p (g u) n -> p g n u", u=2),
-                )
+                nc.scalar.copy(out=ew, in_=xw)
 
         def vpath_pe(inst, cc):
             pr, v = inst // 2, inst % 2
@@ -410,8 +347,8 @@ def tile_window_attention_t_kernel(tc, kv, q, mask, out):
 
         def quant_e(gi):
             g0, gn = groups[gi]
-            ecode[gi] = work.tile([P, 2 * gn * P], U32, name="ecode", tag="ecode", bufs=Q_BUFS, align_bytes=64)
-            escale[gi] = work.tile([P, 2 * gn * P], U8, name="escale", tag="escale", bufs=Q_BUFS, align_bytes=64)
+            ecode[gi] = work.tile([P, 2 * gn * P], U32, name="ecode", tag="ecode", bufs=2, align_bytes=64)
+            escale[gi] = work.tile([P, 2 * gn * P], U8, name="escale", tag="escale", bufs=2, align_bytes=64)
             nc.vector.quantize_mx(
                 out=ecode[gi][:].bitcast(FP8X4),
                 scales=escale[gi][:],
@@ -428,25 +365,30 @@ def tile_window_attention_t_kernel(tc, kv, q, mask, out):
                     identity=ident_f[:],
                 )
             rsb[gi] = work.tile([P, gn * P], F32, name="rsb", tag="rsb", bufs=3)
-            if gi >= RBV_FROM:
-                nc.vector.tensor_copy(out=rsb[gi][:], in_=rp[:])
-            else:
-                nc.scalar.copy(out=rsb[gi][:], in_=rp[:])
+            nc.scalar.copy(out=rsb[gi][:], in_=rp[:])
+
+        def sums_recip(inst):
+            nc.vector.reciprocal(out=rpad[inst % 2][:, 0:8], in_=rsi[inst][:])
+
+        def sums_t(inst):
+            rpt[inst] = ps_t.tile([P, P], F32, name="rpt", tag="t")
+            nc.tensor.transpose(out=rpt[inst][:], in_=rpad[inst % 2][:], identity=ident_f[:])
+
+        def sums_spread(inst):
+            rrow = work.tile([8, P], F32, name="rrow", tag="rrow", bufs=2)
+            nc.scalar.copy(out=rrow[:], in_=rpt[inst][0:8, :])
+            h0 = (inst % 2) * 16
+            rows = out[1, 511 - inst // 2, h0:h0 + 16, :]
+            nc.sync.dma_start(out=rows.rearrange("(t a) w -> t (a w)", a=2), in_=rrow[:])
+            rbt[inst] = work.tile([P, NKEY], F32, name="rb", tag="rb", bufs=2)
+            nc.sync.dma_start(out=rbt[inst][:], in_=rows.rearrange("h w -> (h w)").partition_broadcast(P))
 
         def mx(gi, cc):
             g0, gn = groups[gi]
             inst = g0 // 8
             w = gn * P
-            if TAIL == 2 and g0 >= 60:
-                if cc == 0:
-                    otl[gi] = ps_s.tile([P, 2, w], F32, name="ol%d" % gi, tag="s%d" % ((gi - 14) % 2))
-                ot[(gi, cc)] = otl[gi][:, cc, :]
-            elif TAIL == 1 and gi == len(groups) - 2:
-                o_t = ps_s.tile([P, w], F32, name="os%d" % cc, tag="s%d" % cc)
-                ot[(gi, cc)] = o_t[:]
-            else:
-                o_t = ps_o.tile([P, w], F32, name="o%d" % cc, tag="o%d" % cc)
-                ot[(gi, cc)] = o_t[:]
+            o_t = ps_o.tile([P, w], F32, name="o%d" % cc, tag="o%d" % cc)
+            ot[(gi, cc)] = o_t[:]
             for g in range(2):
                 w0 = g * 256 + cc * P
                 nc.tensor.matmul_mx(
@@ -459,33 +401,43 @@ def tile_window_attention_t_kernel(tc, kv, q, mask, out):
                     stop=(g == 1),
                 )
 
+        def pace(i):
+            hold = work.tile([P, 1], F32, name="hold", tag="hold", bufs=2)
+            nc.gpsimd.tensor_copy(out=hold[:], in_=nmt[i][:])
+
         def on_gp(gi):
             return groups[gi][0] < GP_UNTIL
 
-        def o_out(gi, cc):
+        def oa_part(gi, cc):
             g0, gn = groups[gi]
-            osb[(gi, cc)] = work.tile([P, gn * P], F32, name="osb%d" % cc, tag="osb%d" % cc, bufs=2)
-            nc.scalar.copy(out=osb[(gi, cc)][:], in_=ot[(gi, cc)])
+            pr, v, qt = where(g0)
+            if (pr, cc) not in oa:
+                oa[(pr, cc)] = work.tile([P, 32, 2, 32], F32, name="oa%d" % cc, tag="oa%d" % cc, bufs=2)
+            return oa[(pr, cc)][:, qt * 4:(qt + gn) * 4, v, :]
+
+        def o_out(gi, cc):
+            nc.scalar.copy(out=oa_part(gi, cc), in_=ot[(gi, cc)].rearrange("p (h w) -> p h w", w=32))
+
+        def tr_x(i):
+            transposes(i, 0)
+            transposes(i, 1)
+            evac_tile(i)
 
         def norm_store(gi, cc):
             g0, gn = groups[gi]
             pr, v, qt = where(g0)
             h0, h1 = qt * 4, (qt + gn) * 4
-            if v == 0 and qt == 0:
-                oa[(pr, cc)] = work.tile([P, 32, 2, 32], F32, name="oa%d" % cc, tag="oa%d" % cc, bufs=2)
+            part = oa_part(gi, cc)
+            if by_dma(g0):
+                r = rbt[g0 // 8][:, qt * P:(qt + gn) * P]
+            else:
+                r = rsb[gi][:]
+            r = r.rearrange("p (h w) -> p h w", w=32)
             if on_gp(gi):
-                nc.gpsimd.tensor_tensor(
-                    out=oa[(pr, cc)][:, h0:h1, v, :],
-                    in0=osb[(gi, cc)][:].rearrange("p (h w) -> p h w", w=32),
-                    in1=rsb[gi][:].rearrange("p (h w) -> p h w", w=32),
-                    op=ALU.mult,
-                )
+                nc.gpsimd.tensor_tensor(out=part, in0=part, in1=r, op=ALU.mult)
             else:
                 nc.vector.tensor_tensor(
-                    out=oa[(pr, cc)][:, h0:h1, v, :],
-                    in0=ot[(gi, cc)].rearrange("p (h w) -> p h w", w=32),
-                    in1=rsb[gi][:].rearrange("p (h w) -> p h w", w=32),
-                    op=ALU.mult,
+                    out=part, in0=ot[(gi, cc)].rearrange("p (h w) -> p h w", w=32), in1=r, op=ALU.mult,
                 )
             if v == 1:
                 c0 = chan0(pr, cc)
@@ -519,168 +471,107 @@ def tile_window_attention_t_kernel(tc, kv, q, mask, out):
             for k in range(4):
                 sq_at[16 * (pr - 1) + D_SQ[k]] = (pr, k % 2, k // 2)
 
-        def tr_x(i):
-            transposes(i, 0)
-            transposes(i, 1)
-            evac_tile(i)
-
-        def tail_a():
-            exp_tile(62)
-            row_min(63)
-            tr_x(59)
-            exp_tile(63)
-            tr_x(60)
-            tr_x(61)
-            spread_r(14)
-            mx(13, 1)
-            o_out(13, 1)
-            norm_store(13, 1)
-            quant_e(14)
-            recip(15)
-            tr_x(62)
-            tr_x(63)
-            mx(14, 0)
-            mx(14, 1)
-            quant_e(15)
-            recip(16)
-            recip(17)
-            spread_r(15)
-            norm_store(14, 0)
-            norm_store(14, 1)
-            quant_e(16)
-            quant_e(17)
-            spread_r(16)
-            spread_r(17)
-            for gi in (15, 16, 17):
+        st_at = {}
+        sr_at = {}
+        md_at = {}
+        for inst in range(DMA_INSTS):
+            d_rc, d_rd, d_md = (D_LAST[0], D_LAST[1], D_LAST[2:]) if inst == 6 else (D_RC, D_RD, D_MD5 if inst == 5 else D_MD)
+            st_at[8 * inst + 7 + d_rd] = inst
+            sr_at[8 * inst + 7 + d_rc] = inst
+            for k in range(2):
                 for cc in range(2):
-                    mx(gi, cc)
-            for gi in (15, 16, 17):
-                for cc in range(2):
-                    norm_store(gi, cc)
-
-        def tail():
-            if TAIL_ORDER == 0:
-                tail_a()
-            else:
-                tail_b()
-
-        def tail_b():
-            exp_tile(62)
-            row_min(63)
-            tr_x(59)
-            exp_tile(63)
-            quant_e(14)
-            tr_x(60)
-            tr_x(61)
-            spread_r(14)
-            mx(13, 1)
-            o_out(13, 1)
-            norm_store(13, 1)
-            recip(15)
-            tr_x(62)
-            tr_x(63)
-            mx(14, 0)
-            mx(14, 1)
-            quant_e(15)
-            recip(16)
-            recip(17)
-            spread_r(15)
-            norm_store(14, 0)
-            norm_store(14, 1)
-            quant_e(16)
-            quant_e(17)
-            for cc in range(2):
-                mx(15, cc)
-            spread_r(16)
-            spread_r(17)
-            for gi in (16, 17):
-                for cc in range(2):
-                    mx(gi, cc)
-            for gi in (15, 16, 17):
-                for cc in range(2):
-                    norm_store(gi, cc)
+                    md_at.setdefault(8 * inst + 7 + d_md[k][cc], []).append((2 * inst + k, cc))
 
         load_pair(0)
-        for s in range(NT if TAIL == 2 else NT + T_LAG + 12):
+        for t in rpad:
+            nc.gpsimd.memset(t[:], 0.0)
+        for s in range(NT):
             if s % 16 == 0 and s // 16 + 1 < 4:
                 load_pair(s // 16 + 1)
             j = s - T_LAG
-            e_first = TAIL >= 1 and s >= NT
-            if e_first and 0 <= s - 2 < NT:
-                exp_tile(s - 2)
             if s < NT:
                 scores(s, 0)
-            if MX_EARLY:
-                for cc in range(2):
-                    gi = half_at(s, D_MX, cc)
-                    if gi is not None:
-                        mx(gi, cc)
-                        if on_gp(gi):
-                            o_out(gi, cc)
-            if 0 <= j < NT:
+            due = [(half_at(s, D_MX, cc), cc) for cc in range(2) if half_at(s, D_MX, cc) is not None]
+
+            def sums():
+                for gi, cc in due:
+                    mx(gi, cc)
+
+            if j >= 0:
                 transposes(j, 0)
-                if TR_MODE >= 1:
-                    transposes(j, 1)
-                    evac_tile(j)
-            if TR_MODE == 2:
-                for cc in range(2):
-                    if (s, cc) in vt_at:
-                        vpath_pe(vt_at[(s, cc)], cc)
-                if grp_at(s, D_RS) is not None:
-                    spread_r(grp_at(s, D_RS))
-            if s < NT:
-                scores(s, 1)
-            for cc in range(2):
-                if half_at(s, D_MX, cc) is not None and not MX_EARLY:
-                    mx(half_at(s, D_MX, cc), cc)
-            if 0 <= j < NT and TR_MODE == 0:
+            scores(s, 1, sums)
+            for gi, cc in due:
+                if on_gp(gi):
+                    o_out(gi, cc)
+            if j >= 0:
                 transposes(j, 1)
                 evac_tile(j)
-            if TR_MODE < 2:
-                for cc in range(2):
-                    if (s, cc) in vt_at:
-                        vpath_pe(vt_at[(s, cc)], cc)
-                if grp_at(s, D_RS) is not None:
-                    spread_r(grp_at(s, D_RS))
-            if s < NT and on_ar(s):
-                for nh in range(2):
-                    ar_copy(s, nh)
-                for nh in range(2):
-                    ar_add(s, nh)
-            if 0 <= s - 2 < NT and not on_ar(s - 2) and not O_FIRST and not e_first:
-                exp_tile(s - 2)
             for cc in range(2):
-                gi = half_at(s, D_O, cc)
-                if gi is not None and on_gp(gi) and not MX_EARLY:
-                    o_out(gi, cc)
-            if 0 <= s - 2 < NT and not on_ar(s - 2) and O_FIRST and not e_first:
+                if (s, cc) in vt_at:
+                    vpath_pe(vt_at[(s, cc)], cc)
+            if s in st_at:
+                sums_t(st_at[s])
+                sums_spread(st_at[s])
+            gi = grp_at(s, D_RS)
+            if gi is not None and not by_dma(groups[gi][0]):
+                spread_r(gi)
+            if 0 <= s - 2 < NT:
                 exp_tile(s - 2)
-            first = HEAD >= 1 and s == 1
-            if first:
-                row_min(0)
-            if s < NT and not on_ar(s):
+            if s < NT:
                 leave_psum(s, 0)
-            late = 0 <= s - 2 < NT and on_ar(s - 2)
-            if late:
-                row_min(s - 2)
-                exp_tile(s - 2)
-            if 0 <= s - 1 < NT and not on_ar(s - 1) and not late and not first:
+            if 0 <= s - 1 < NT:
                 row_min(s - 1)
-            if s < NT and not on_ar(s):
+            if s < NT:
                 leave_psum(s, 1)
-            if late:
-                row_min(s - 1)
             if s in vq_at:
                 vpath_q(vq_at[s])
-            if grp_at(s, D_RC) is not None:
-                recip(grp_at(s, D_RC))
+            if s in sr_at:
+                sums_recip(sr_at[s])
+            gi = grp_at(s, D_RC)
+            if gi is not None and not by_dma(groups[gi][0]):
+                recip(gi)
             if grp_at(s, D_QE) is not None:
                 quant_e(grp_at(s, D_QE))
             for cc in range(2):
                 gi = half_at(s, D_M, cc)
-                if gi is not None:
+                if gi is not None and not by_dma(groups[gi][0]):
                     norm_store(gi, cc)
+            for gi, cc in md_at.get(s, []):
+                pace(max(i for i in range(s) if i in nmt))
+                norm_store(gi, cc)
+            if s + MT_LEAD in MT_SET:
+                build_mt(s + MT_LEAD)
             if s in sq_at:
                 scale_q(sq_at[s][0], sq_at[s][1], sq_at[s][2], 0, 32)
-        if TAIL == 2:
-            tail()
+        exp_tile(62)
+        row_min(63)
+        mx(13, 1)
+        tr_x(59)
+        exp_tile(63)
+        recip(14)
+        norm_store(13, 0)
+        norm_store(13, 1)
+        quant_e(14)
+        spread_r(14)
+        tr_x(60)
+        tr_x(61)
+        recip(15)
+        spread_r(15)
+        tr_x(62)
+        mx(14, 0)
+        mx(14, 1)
+        tr_x(63)
+        recip(16)
+        quant_e(15)
+        spread_r(16)
+        norm_store(14, 0)
+        norm_store(14, 1)
+        mx(15, 0)
+        mx(15, 1)
+        quant_e(16)
+        mx(16, 0)
+        mx(16, 1)
+        norm_store(15, 0)
+        norm_store(15, 1)
+        norm_store(16, 0)
+        norm_store(16, 1)

@@ -19,11 +19,12 @@ FLOPS = 2 * 2 * 8 * 1024 * 1024 * 256
 
 T_LAG = 5
 E_BUFS = 5
-U_BUFS = 7
+U_BUFS = 5
 PE_MASK = (2, 7, 12)
 MT_SET = (4, 9, 14)
 MT_LEAD = 2
-MT_FROM = 5
+MT_FIRST = 5
+MT_FROM = 8
 MT_V = ()
 LAST_SPLIT = (2, 2)
 GP_UNTIL = 52
@@ -34,14 +35,17 @@ D_RS = 7
 D_MX = (8, 9)
 D_M = (8, 9)
 D_LAST = (3, 4, (7, 8), (99, 99))
-D_MD5 = ((12, 12), (13, 14))
-V_EVAC = (59, 60)
+D_MD5 = ((11, 12), (12, 13))
+V_EVAC = (61,)
 TAIL_S = (60, 61, 62, 63)
 D_RD = 7
 D_MD = ((12, 13), (16, 17))
 D_VT = (0, 4)
 D_QV = 5
-D_SQ = (7, 11, 15, 19)
+D_SQ = (6, 10, 14, 18)
+D_PV = (-5, -1)
+PV_FIRST = 3
+SQ0 = 4
 
 
 def tile_window_attention_t_kernel(tc, kv, q, mask, out):
@@ -83,6 +87,7 @@ def tile_window_attention_t_kernel(tc, kv, q, mask, out):
         qd = {}
         qs = {}
         vd = {}
+        vraw = {}
         oa = {}
         vcode = {}
         vscale = {}
@@ -105,6 +110,9 @@ def tile_window_attention_t_kernel(tc, kv, q, mask, out):
         ot = {}
         mt = {}
 
+        def half(nh):
+            return slice(nh * 512, (nh + 1) * 512)
+
         def chan0(pr, cc):
             return (pr % 2) * 256 + cc * P
 
@@ -121,11 +129,19 @@ def tile_window_attention_t_kernel(tc, kv, q, mask, out):
         def load_q(pr, cc, h0, h1):
             load_rows(qd[(pr, cc)], q[pr // 2], pr, cc, h0, h1)
 
-        def load_v(pr, cc, v):
-            c0 = chan0(pr, cc)
-            nc.sync.dma_start(
-                out=vd[(pr, cc, v)][:].rearrange("c (h w) -> c h w", w=32),
-                in_=kv[1, pr // 2, c0:c0 + P, :, v * 32:(v + 1) * 32],
+        def load_v(pr, cc):
+            load_rows(vraw[(pr, cc)], kv[1, pr // 2], pr, cc, 0, 32)
+
+        def pick_v(inst, cc):
+            pr, v = inst // 2, inst % 2
+            vd[(inst, cc)] = work.tile([P, NKEY], BF16, name="vd%d" % cc, tag="vd%d" % cc, bufs=2)
+            nc.gpsimd.tensor_scalar(
+                out=vd[(inst, cc)][:].rearrange("c (h w) -> c h w", w=32),
+                in0=vraw[(pr, cc)][:].rearrange("c (h v w) -> c h v w", v=2, w=32)[:, :, v, :],
+                scalar1=1.0,
+                scalar2=0.0,
+                op0=ALU.mult,
+                op1=ALU.add,
             )
 
         def scale_q(pr, cc, v, h0, h1):
@@ -145,47 +161,48 @@ def tile_window_attention_t_kernel(tc, kv, q, mask, out):
                 in_=mask[v, t0 * P:(t0 + n) * P, :].rearrange("(t p) k -> p t k", p=P),
             )
 
+        def load_mask_half(nh):
+            nc.sync.dma_start(
+                out=mask_sb[0][:, 0:2, half(nh)],
+                in_=mask[0, 0:2 * P, half(nh)].rearrange("(t p) k -> p t k", p=P),
+            )
+
         def load_pair(pr):
             for cc in range(2):
                 kraw[(pr, cc)] = inp.tile([P, 2048], BF16, name="kraw%d" % cc, tag="kraw%d" % cc)
                 qd[(pr, cc)] = inp.tile([P, 2048], BF16, name="qd%d" % cc, tag="qd%d" % cc)
+                vraw[(pr, cc)] = inp.tile([P, 2048], BF16, name="vraw%d" % cc, tag="vraw%d" % cc)
                 for v in range(2):
                     qs[(pr, cc, v)] = inp.tile([P, NKEY], BF16, name="qs%d%d" % (cc, v), tag="qs%d%d" % (cc, v))
-                    vd[(pr, cc, v)] = inp.tile([P, NKEY], BF16, name="vd%d%d" % (cc, v), tag="vd%d%d" % (cc, v))
             if pr == 0:
                 for cc in range(2):
-                    load_q(pr, cc, 0, 4)
-                    scale_q(pr, cc, 0, 0, 4)
+                    load_q(pr, cc, 0, 8)
+                    scale_q(pr, cc, 0, 0, 8)
                 for cc in range(2):
                     load_k(pr, cc, 0, 16)
-                load_mask(0, 0, 1)
+                load_mask_half(0)
                 for cc in range(2):
                     load_k(pr, cc, 16, 32)
-                for cc in range(2):
-                    load_q(pr, cc, 4, 16)
-                    scale_q(pr, cc, 0, 4, 16)
-                load_mask(0, 1, 1)
+                load_mask_half(1)
                 load_mask(0, 2, 2)
+                for cc in range(2):
+                    load_q(pr, cc, 8, 16)
+                    scale_q(pr, cc, 0, 8, 16)
                 for cc in range(2):
                     load_q(pr, cc, 16, 32)
                     scale_q(pr, cc, 0, 16, 32)
                 load_mask(0, 4, 4)
                 for cc in range(2):
-                    load_v(pr, cc, 0)
-                for cc in range(2):
-                    scale_q(pr, cc, 1, 0, 32)
+                    load_v(pr, cc)
                 load_mask(1, 0, 4)
-                for cc in range(2):
-                    load_v(pr, cc, 1)
                 load_mask(1, 4, 4)
             else:
                 for cc in range(2):
                     load_k(pr, cc, 0, 32)
                 for cc in range(2):
                     load_q(pr, cc, 0, 32)
-                for v in range(2):
-                    for cc in range(2):
-                        load_v(pr, cc, v)
+                for cc in range(2):
+                    load_v(pr, cc)
 
         def where(i):
             inst = i // 8
@@ -205,9 +222,6 @@ def tile_window_attention_t_kernel(tc, kv, q, mask, out):
 
         def flat(ap):
             return ap.rearrange("q (u p e) -> q u p e", u=2, e=2)
-
-        def half(nh):
-            return slice(nh * 512, (nh + 1) * 512)
 
         def scores(i, nh, between=None):
             pr, v, qt = where(i)
@@ -317,11 +331,10 @@ def tile_window_attention_t_kernel(tc, kv, q, mask, out):
                 nc.scalar.copy(out=ew, in_=xw)
 
         def vpath_pe(inst, cc):
-            pr, v = inst // 2, inst % 2
             if inst not in gvt:
                 gvt[inst] = work.tile([P, 2, 256, 4], BF16, name="gv", tag="gv", bufs=2, align_bytes=64)
             gwords = gvt[inst][:].rearrange("p g c t -> p (g c t)").bitcast(F32).rearrange("p (g c u) -> p g c u", g=2, u=2)
-            vwords = vd[(pr, cc, v)][:].bitcast(F32)
+            vwords = vd[(inst, cc)][:].bitcast(F32)
             vt = ps_t.tile([P, 4, P], F32, name="vt", tag="t")
             for g in range(2):
                 for uu in range(2):
@@ -470,6 +483,12 @@ def tile_window_attention_t_kernel(tc, kv, q, mask, out):
         for pr in range(1, 4):
             for k in range(4):
                 sq_at[16 * (pr - 1) + D_SQ[k]] = (pr, k % 2, k // 2)
+        sq_at[SQ0] = (0, 0, 1)
+        sq_at[SQ0 + 1] = (0, 1, 1)
+        pv_at = {}
+        for inst in range(8):
+            for cc in range(2):
+                pv_at.setdefault(max(8 * inst + D_PV[cc], PV_FIRST + cc), []).append((inst, cc))
 
         st_at = {}
         sr_at = {}
@@ -489,8 +508,10 @@ def tile_window_attention_t_kernel(tc, kv, q, mask, out):
             if s % 16 == 0 and s // 16 + 1 < 4:
                 load_pair(s // 16 + 1)
             j = s - T_LAG
-            if s < NT:
+            if s != 1:
                 scores(s, 0)
+            if s == 0:
+                scores(1, 0)
             due = [(half_at(s, D_MX, cc), cc) for cc in range(2) if half_at(s, D_MX, cc) is not None]
 
             def sums():
@@ -517,8 +538,10 @@ def tile_window_attention_t_kernel(tc, kv, q, mask, out):
                 spread_r(gi)
             if 0 <= s - 2 < NT:
                 exp_tile(s - 2)
-            if s < NT:
+            if s != 1:
                 leave_psum(s, 0)
+            if s == 0:
+                leave_psum(1, 0)
             if 0 <= s - 1 < NT:
                 row_min(s - 1)
             if s < NT:
@@ -536,11 +559,15 @@ def tile_window_attention_t_kernel(tc, kv, q, mask, out):
                 gi = half_at(s, D_M, cc)
                 if gi is not None and not by_dma(groups[gi][0]):
                     norm_store(gi, cc)
-            for gi, cc in md_at.get(s, []):
+            if s > 2 and (s in md_at or s in pv_at or s in sq_at):
                 pace(max(i for i in range(s) if i in nmt))
+            for gi, cc in md_at.get(s, []):
                 norm_store(gi, cc)
-            if s + MT_LEAD in MT_SET:
-                build_mt(s + MT_LEAD)
+            for inst, cc in pv_at.get(s, []):
+                pick_v(inst, cc)
+            for k in MT_SET:
+                if s == max(k - MT_LEAD, MT_FIRST):
+                    build_mt(k)
             if s in sq_at:
                 scale_q(sq_at[s][0], sq_at[s][1], sq_at[s][2], 0, 32)
         exp_tile(62)
@@ -548,21 +575,21 @@ def tile_window_attention_t_kernel(tc, kv, q, mask, out):
         mx(13, 1)
         tr_x(59)
         exp_tile(63)
-        recip(14)
         norm_store(13, 0)
-        norm_store(13, 1)
         quant_e(14)
-        spread_r(14)
-        tr_x(60)
-        tr_x(61)
+        recip(14)
         recip(15)
-        spread_r(15)
-        tr_x(62)
+        norm_store(13, 1)
+        tr_x(60)
+        spread_r(14)
+        tr_x(61)
         mx(14, 0)
         mx(14, 1)
+        tr_x(62)
+        quant_e(15)
         tr_x(63)
         recip(16)
-        quant_e(15)
+        spread_r(15)
         spread_r(16)
         norm_store(14, 0)
         norm_store(14, 1)

@@ -36,8 +36,7 @@ D_MX = (8, 9)
 D_M = (8, 9)
 D_LAST = (3, 4, (7, 8), (99, 99))
 D_MD5 = ((11, 12), (12, 13))
-V_EVAC = (61,)
-TAIL_S = (60, 61, 62, 63)
+V_EVAC = (59,)
 D_RD = 7
 D_MD = ((12, 13), (16, 17))
 D_VT = (0, 4)
@@ -56,7 +55,7 @@ def tile_window_attention_t_kernel(tc, kv, q, mask, out):
         inp = ctx.enter_context(tc.tile_pool(name="inp", bufs=2))
         work = ctx.enter_context(tc.tile_pool(name="work", bufs=2))
         ps_s = ctx.enter_context(tc.psum_pool(name="ps_s", bufs=2))
-        ps_t = ctx.enter_context(tc.psum_pool(name="ps_t", bufs=2))
+        ps_t = ctx.enter_context(tc.psum_pool(name="ps_t", bufs=3))
         ps_o = ctx.enter_context(tc.psum_pool(name="ps_o", bufs=1))
         ctx.enter_context(tc.manual_schedule())
 
@@ -248,9 +247,7 @@ def tile_window_attention_t_kernel(tc, kv, q, mask, out):
                 nc.tensor.matmul(out=s_nh[:], lhsT=identm[:], rhs=mask_sb[v][:, qt, half(nh)], start=False, stop=True)
 
         def transposes(i, part):
-            if part == 0 and i in TAIL_S:
-                xtt[i] = ps_s.tile([P, 4, P], F32, name="xs%d" % (i % 2), tag="s%d" % (i % 2))
-            elif part == 0:
+            if part == 0:
                 xtt[i] = ps_t.tile([P, 4, P], F32, name="xt", tag="t")
             ewords = et[i][:].bitcast(F32)
             for kb in range(2 * part, 2 * part + 2):
@@ -370,7 +367,10 @@ def tile_window_attention_t_kernel(tc, kv, q, mask, out):
 
         def spread_r(gi):
             g0, gn = groups[gi]
-            rp = ps_t.tile([P, gn * P], F32, name="rp", tag="t")
+            if g0 >= 56:
+                rp = ps_s.tile([P, gn * P], F32, name="rp%d" % (gi % 2), tag="s%d" % (gi % 2))
+            else:
+                rp = ps_t.tile([P, gn * P], F32, name="rp", tag="t")
             for jj in range(gn):
                 nc.tensor.transpose(
                     out=rp[:, jj * P:(jj + 1) * P],
@@ -400,7 +400,10 @@ def tile_window_attention_t_kernel(tc, kv, q, mask, out):
             g0, gn = groups[gi]
             inst = g0 // 8
             w = gn * P
-            o_t = ps_o.tile([P, w], F32, name="o%d" % cc, tag="o%d" % cc)
+            if g0 + cc >= 53:
+                o_t = ps_s.tile([P, w], F32, name="os%d" % cc, tag="s%d" % cc)
+            else:
+                o_t = ps_o.tile([P, w], F32, name="o", tag="o")
             ot[(gi, cc)] = o_t[:]
             for g in range(2):
                 w0 = g * 256 + cc * P
@@ -570,35 +573,35 @@ def tile_window_attention_t_kernel(tc, kv, q, mask, out):
                     build_mt(k)
             if s in sq_at:
                 scale_q(sq_at[s][0], sq_at[s][1], sq_at[s][2], 0, 32)
+        norm_store(13, 0)
+        tr_x(59)
         exp_tile(62)
         row_min(63)
-        mx(13, 1)
-        tr_x(59)
-        exp_tile(63)
-        norm_store(13, 0)
         quant_e(14)
         recip(14)
         recip(15)
-        norm_store(13, 1)
         tr_x(60)
-        spread_r(14)
+        mx(13, 1)
         tr_x(61)
-        mx(14, 0)
-        mx(14, 1)
+        exp_tile(63)
+        norm_store(13, 1)
         tr_x(62)
+        spread_r(14)
+        mx(14, 0)
         quant_e(15)
+        mx(14, 1)
         tr_x(63)
         recip(16)
-        spread_r(15)
-        spread_r(16)
         norm_store(14, 0)
+        spread_r(15)
         norm_store(14, 1)
         mx(15, 0)
         mx(15, 1)
+        spread_r(16)
         quant_e(16)
-        mx(16, 0)
-        mx(16, 1)
         norm_store(15, 0)
         norm_store(15, 1)
+        mx(16, 0)
+        mx(16, 1)
         norm_store(16, 0)
         norm_store(16, 1)

@@ -42,8 +42,6 @@ D_MD = ((12, 13), (16, 17))
 D_VT = (0, 4)
 D_QV = 5
 D_SQ = (6, 10, 14, 18)
-D_PV = (-5, -1)
-PV_FIRST = 3
 SQ0 = 4
 
 
@@ -86,7 +84,6 @@ def tile_window_attention_t_kernel(tc, kv, q, mask, out):
         qd = {}
         qs = {}
         vd = {}
-        vraw = {}
         oa = {}
         vcode = {}
         vscale = {}
@@ -128,19 +125,13 @@ def tile_window_attention_t_kernel(tc, kv, q, mask, out):
         def load_q(pr, cc, h0, h1):
             load_rows(qd[(pr, cc)], q[pr // 2], pr, cc, h0, h1)
 
-        def load_v(pr, cc):
-            load_rows(vraw[(pr, cc)], kv[1, pr // 2], pr, cc, 0, 32)
-
-        def pick_v(inst, cc):
+        def load_v(inst, cc):
             pr, v = inst // 2, inst % 2
-            vd[(inst, cc)] = work.tile([P, NKEY], BF16, name="vd%d" % cc, tag="vd%d" % cc, bufs=2)
-            nc.gpsimd.tensor_scalar(
+            c0 = chan0(pr, cc)
+            vd[(inst, cc)] = inp.tile([P, NKEY], BF16, name="vd%d%d" % (cc, v), tag="vd%d%d" % (cc, v))
+            nc.sync.dma_start(
                 out=vd[(inst, cc)][:].rearrange("c (h w) -> c h w", w=32),
-                in0=vraw[(pr, cc)][:].rearrange("c (h v w) -> c h v w", v=2, w=32)[:, :, v, :],
-                scalar1=1.0,
-                scalar2=0.0,
-                op0=ALU.mult,
-                op1=ALU.add,
+                in_=kv[1, pr // 2, c0:c0 + P, :, v * 32:(v + 1) * 32],
             )
 
         def scale_q(pr, cc, v, h0, h1):
@@ -170,7 +161,6 @@ def tile_window_attention_t_kernel(tc, kv, q, mask, out):
             for cc in range(2):
                 kraw[(pr, cc)] = inp.tile([P, 2048], BF16, name="kraw%d" % cc, tag="kraw%d" % cc)
                 qd[(pr, cc)] = inp.tile([P, 2048], BF16, name="qd%d" % cc, tag="qd%d" % cc)
-                vraw[(pr, cc)] = inp.tile([P, 2048], BF16, name="vraw%d" % cc, tag="vraw%d" % cc)
                 for v in range(2):
                     qs[(pr, cc, v)] = inp.tile([P, NKEY], BF16, name="qs%d%d" % (cc, v), tag="qs%d%d" % (cc, v))
             if pr == 0:
@@ -192,16 +182,19 @@ def tile_window_attention_t_kernel(tc, kv, q, mask, out):
                     scale_q(pr, cc, 0, 16, 32)
                 load_mask(0, 4, 4)
                 for cc in range(2):
-                    load_v(pr, cc)
+                    load_v(0, cc)
                 load_mask(1, 0, 4)
+                for cc in range(2):
+                    load_v(1, cc)
                 load_mask(1, 4, 4)
             else:
                 for cc in range(2):
                     load_k(pr, cc, 0, 32)
                 for cc in range(2):
                     load_q(pr, cc, 0, 32)
-                for cc in range(2):
-                    load_v(pr, cc)
+                for v in range(2):
+                    for cc in range(2):
+                        load_v(2 * pr + v, cc)
 
         def where(i):
             inst = i // 8
@@ -488,10 +481,6 @@ def tile_window_attention_t_kernel(tc, kv, q, mask, out):
                 sq_at[16 * (pr - 1) + D_SQ[k]] = (pr, k % 2, k // 2)
         sq_at[SQ0] = (0, 0, 1)
         sq_at[SQ0 + 1] = (0, 1, 1)
-        pv_at = {}
-        for inst in range(8):
-            for cc in range(2):
-                pv_at.setdefault(max(8 * inst + D_PV[cc], PV_FIRST + cc), []).append((inst, cc))
 
         st_at = {}
         sr_at = {}
@@ -562,12 +551,10 @@ def tile_window_attention_t_kernel(tc, kv, q, mask, out):
                 gi = half_at(s, D_M, cc)
                 if gi is not None and not by_dma(groups[gi][0]):
                     norm_store(gi, cc)
-            if s > 2 and (s in md_at or s in pv_at or s in sq_at):
+            if s > 2 and (s in md_at or s in sq_at):
                 pace(max(i for i in range(s) if i in nmt))
             for gi, cc in md_at.get(s, []):
                 norm_store(gi, cc)
-            for inst, cc in pv_at.get(s, []):
-                pick_v(inst, cc)
             for k in MT_SET:
                 if s == max(k - MT_LEAD, MT_FIRST):
                     build_mt(k)

@@ -23,7 +23,7 @@ U_BUFS = 5
 PE_MASK = (2, 7, 12)
 MT_SET = (4, 9, 14)
 MT_LEAD = 2
-MT_FIRST = 5
+MT_FIRST = 4
 MT_FROM = 8
 MT_V = ()
 LAST_SPLIT = (2, 2)
@@ -31,7 +31,6 @@ GP_UNTIL = 52
 DMA_INSTS = 7
 D_QE = 6
 D_RC = 6
-D_RS = 7
 D_MX = (8, 9)
 D_M = (8, 9)
 D_LAST = (3, 4, (7, 8), (99, 99))
@@ -525,26 +524,23 @@ def tile_window_attention_t_kernel(tc, kv, q, mask, out):
             if s in st_at:
                 sums_t(st_at[s])
                 sums_spread(st_at[s])
-            gi = grp_at(s, D_RS)
-            if gi is not None and not by_dma(groups[gi][0]):
-                spread_r(gi)
+            if s == 62:
+                spread_r(14)
             if 0 <= s - 2 < NT:
                 exp_tile(s - 2)
+            if s == 2:
+                row_min(1)
             if s != 1:
                 leave_psum(s, 0)
             if s == 0:
                 leave_psum(1, 0)
-            if 0 <= s - 1 < NT:
+            if s >= 1 and s != 2:
                 row_min(s - 1)
-            if s < NT:
-                leave_psum(s, 1)
+            leave_psum(s, 1)
             if s in vq_at:
                 vpath_q(vq_at[s])
             if s in sr_at:
                 sums_recip(sr_at[s])
-            gi = grp_at(s, D_RC)
-            if gi is not None and not by_dma(groups[gi][0]):
-                recip(gi)
             if grp_at(s, D_QE) is not None:
                 quant_e(grp_at(s, D_QE))
             for cc in range(2):
@@ -553,6 +549,8 @@ def tile_window_attention_t_kernel(tc, kv, q, mask, out):
                     norm_store(gi, cc)
             if s > 2 and (s in md_at or s in sq_at):
                 pace(max(i for i in range(s) if i in nmt))
+            if s == 61:
+                recip(14)
             for gi, cc in md_at.get(s, []):
                 norm_store(gi, cc)
             for k in MT_SET:
@@ -560,32 +558,30 @@ def tile_window_attention_t_kernel(tc, kv, q, mask, out):
                     build_mt(k)
             if s in sq_at:
                 scale_q(sq_at[s][0], sq_at[s][1], sq_at[s][2], 0, 32)
-        norm_store(13, 0)
-        tr_x(59)
+        mx(13, 1)
         exp_tile(62)
         row_min(63)
+        tr_x(59)
+        exp_tile(63)
         quant_e(14)
-        recip(14)
         recip(15)
         tr_x(60)
-        mx(13, 1)
         tr_x(61)
-        exp_tile(63)
-        norm_store(13, 1)
+        norm_store(13, 0)
         tr_x(62)
-        spread_r(14)
         mx(14, 0)
-        quant_e(15)
         mx(14, 1)
         tr_x(63)
-        recip(16)
+        norm_store(13, 1)
         norm_store(14, 0)
-        spread_r(15)
         norm_store(14, 1)
+        quant_e(15)
+        recip(16)
+        spread_r(15)
         mx(15, 0)
         mx(15, 1)
-        spread_r(16)
         quant_e(16)
+        spread_r(16)
         norm_store(15, 0)
         norm_store(15, 1)
         mx(16, 0)

@@ -23,7 +23,7 @@ U_BUFS = 5
 PE_MASK = (2, 7, 12)
 MT_SET = (4, 9, 14)
 MT_LEAD = 2
-MT_FIRST = 4
+MT_FIRST = 7
 MT_FROM = 8
 MT_V = ()
 LAST_SPLIT = (2, 2)
@@ -172,10 +172,10 @@ def tile_window_attention_t_kernel(tc, kv, q, mask, out):
                 for cc in range(2):
                     load_k(pr, cc, 16, 32)
                 load_mask_half(1)
-                load_mask(0, 2, 2)
                 for cc in range(2):
                     load_q(pr, cc, 8, 16)
                     scale_q(pr, cc, 0, 8, 16)
+                load_mask(0, 2, 2)
                 for cc in range(2):
                     load_q(pr, cc, 16, 32)
                     scale_q(pr, cc, 0, 16, 32)
@@ -524,14 +524,14 @@ def tile_window_attention_t_kernel(tc, kv, q, mask, out):
             if s in st_at:
                 sums_t(st_at[s])
                 sums_spread(st_at[s])
-            if s == 62:
-                spread_r(14)
             if 0 <= s - 2 < NT:
                 exp_tile(s - 2)
             if s == 2:
                 row_min(1)
             if s != 1:
                 leave_psum(s, 0)
+            if s == 62:
+                recip(14)
             if s == 0:
                 leave_psum(1, 0)
             if s >= 1 and s != 2:
@@ -549,8 +549,6 @@ def tile_window_attention_t_kernel(tc, kv, q, mask, out):
                     norm_store(gi, cc)
             if s > 2 and (s in md_at or s in sq_at):
                 pace(max(i for i in range(s) if i in nmt))
-            if s == 61:
-                recip(14)
             for gi, cc in md_at.get(s, []):
                 norm_store(gi, cc)
             for k in MT_SET:
@@ -559,6 +557,7 @@ def tile_window_attention_t_kernel(tc, kv, q, mask, out):
             if s in sq_at:
                 scale_q(sq_at[s][0], sq_at[s][1], sq_at[s][2], 0, 32)
         mx(13, 1)
+        spread_r(14)
         exp_tile(62)
         row_min(63)
         tr_x(59)

@@ -37,7 +37,7 @@ D_LAST = (3, 4, (7, 8), (99, 99))
 D_MD5 = ((11, 12), (12, 13))
 V_EVAC = (59,)
 D_RD = 7
-D_MD = ((12, 13), (16, 17))
+D_MD = ((11, 11), (15, 15))
 D_VT = (0, 4)
 D_QV = 5
 D_SQ = (6, 10, 14, 18)
@@ -411,7 +411,7 @@ def tile_window_attention_t_kernel(tc, kv, q, mask, out):
 
         def pace(i):
             hold = work.tile([P, 1], F32, name="hold", tag="hold", bufs=2)
-            nc.gpsimd.tensor_copy(out=hold[:], in_=nmt[i][:])
+            nc.gpsimd.tensor_copy(out=hold[:], in_=ut[i][:, 0:1])
 
         def on_gp(gi):
             return groups[gi][0] < GP_UNTIL
@@ -487,7 +487,8 @@ def tile_window_attention_t_kernel(tc, kv, q, mask, out):
         for inst in range(DMA_INSTS):
             d_rc, d_rd, d_md = (D_LAST[0], D_LAST[1], D_LAST[2:]) if inst == 6 else (D_RC, D_RD, D_MD5 if inst == 5 else D_MD)
             st_at[8 * inst + 7 + d_rd] = inst
-            sr_at[8 * inst + 7 + d_rc] = inst
+            if inst < 6:
+                sr_at[8 * inst + 7 + d_rc] = inst
             for k in range(2):
                 for cc in range(2):
                     md_at.setdefault(8 * inst + 7 + d_md[k][cc], []).append((2 * inst + k, cc))
@@ -528,6 +529,8 @@ def tile_window_attention_t_kernel(tc, kv, q, mask, out):
                 exp_tile(s - 2)
             if s == 2:
                 row_min(1)
+            if s == 55 + D_LAST[0]:
+                sums_recip(6)
             if s != 1:
                 leave_psum(s, 0)
             if s == 62:
@@ -548,7 +551,7 @@ def tile_window_attention_t_kernel(tc, kv, q, mask, out):
                 if gi is not None and not by_dma(groups[gi][0]):
                     norm_store(gi, cc)
             if s > 2 and (s in md_at or s in sq_at):
-                pace(max(i for i in range(s) if i in nmt))
+                pace(s)
             for gi, cc in md_at.get(s, []):
                 norm_store(gi, cc)
             for k in MT_SET:

@@ -23,7 +23,7 @@ U_BUFS = 5
 PE_MASK = (2, 7, 12)
 MT_SET = (4, 9, 14)
 MT_LEAD = 2
-MT_FIRST = 7
+MT_FIRST = 5
 MT_FROM = 8
 MT_V = ()
 LAST_SPLIT = (2, 2)
@@ -199,14 +199,14 @@ def tile_window_attention_t_kernel(tc, kv, q, mask, out):
             inst = i // 8
             return inst // 2, inst % 2, i % 8
 
-        def on_pe(i):
-            return i % 16 in PE_MASK
+        def on_pe(i, nh):
+            return i % 16 in PE_MASK or i == NT - 1 and nh == 1
 
         def on_mt(i):
             return i >= MT_FROM and i % 16 in MT_SET
 
-        def in_psum(i):
-            return on_pe(i) or on_mt(i)
+        def in_psum(i, nh):
+            return on_pe(i, nh) or on_mt(i)
 
         def perm(ap):
             return ap.rearrange("q (p u e) -> q u p e", u=2, e=2)
@@ -227,7 +227,7 @@ def tile_window_attention_t_kernel(tc, kv, q, mask, out):
                     lhsT=qs[(pr, cc, v)][:, qt * P:(qt + 1) * P],
                     rhs=kview[:, nh * 16:(nh + 1) * 16, v, :],
                     start=(cc == 0),
-                    stop=(cc == 1 and not in_psum(i)),
+                    stop=(cc == 1 and not in_psum(i, nh)),
                 )
             if on_mt(i):
                 for kb in range(4):
@@ -235,7 +235,7 @@ def tile_window_attention_t_kernel(tc, kv, q, mask, out):
                         out=s_nh[:, kb * P:(kb + 1) * P], lhsT=mt[i % 16][:, 4 * nh + kb, :], rhs=ident_f[:],
                         is_transpose=True, start=False, stop=(kb == 3),
                     )
-            if on_pe(i):
+            if on_pe(i, nh):
                 nc.tensor.matmul(out=s_nh[:], lhsT=identm[:], rhs=mask_sb[v][:, qt, half(nh)], start=False, stop=True)
 
         def transposes(i, part):
@@ -249,16 +249,16 @@ def tile_window_attention_t_kernel(tc, kv, q, mask, out):
             pr, v, qt = where(i)
             if nh == 0:
                 ut[i] = work.tile([P, NKEY], F32, name="u", tag="u", bufs=U_BUFS)
-                if in_psum(i):
+                if in_psum(i, 1):
                     nm2t[i] = work.tile([P, 1], F32, name="nm2", tag="nm2", bufs=2)
             u = ut[i]
-            if in_psum(i) and nh == 1:
+            if in_psum(i, nh) and nh == 1:
                 nmt[i] = work.tile([P, 1], F32, name="nm", tag="nm", bufs=6)
                 nc.vector.tensor_scalar(
                     out=flat(u[:, half(nh)]), in0=perm(st[(i, nh)][:]), scalar1=1.0, scalar2=nm2t[i][:],
                     op0=ALU.mult, op1=ALU.min, accum_out=nmt[i][:],
                 )
-            elif in_psum(i):
+            elif in_psum(i, nh):
                 nc.vector.tensor_scalar(
                     out=flat(u[:, half(nh)]), in0=perm(st[(i, nh)][:]), scalar1=1.0, scalar2=None,
                     op0=ALU.mult, op1=ALU.min, accum_out=nm2t[i][:],
@@ -268,6 +268,8 @@ def tile_window_attention_t_kernel(tc, kv, q, mask, out):
                     out=flat(u[:, half(nh)]), in0=perm(st[(i, nh)][:]), in1=perm(mask_sb[v][:, qt, half(nh)]),
                     op=ALU.subtract,
                 )
+                if nh == 0 and in_psum(i, 1):
+                    nc.vector.tensor_reduce(out=nm2t[i][:], in_=u[:, half(0)], axis=AX.X, op=ALU.min)
 
         def build_mt(k):
             v, qt = k // 8, k % 8
@@ -281,7 +283,7 @@ def tile_window_attention_t_kernel(tc, kv, q, mask, out):
                 nc.scalar.activation(out=mt[k][:], in_=pt[:], func=ACT.Copy, scale=-1.0)
 
         def row_min(i):
-            if in_psum(i):
+            if in_psum(i, 1):
                 return
             nm = work.tile([P, 1], F32, name="nm", tag="nm", bufs=6)
             nmt[i] = nm
@@ -510,13 +512,12 @@ def tile_window_attention_t_kernel(tc, kv, q, mask, out):
                 for gi, cc in due:
                     mx(gi, cc)
 
-            if j >= 0:
-                transposes(j, 0)
             scores(s, 1, sums)
             for gi, cc in due:
                 if on_gp(gi):
                     o_out(gi, cc)
             if j >= 0:
+                transposes(j, 0)
                 transposes(j, 1)
                 evac_tile(j)
             for cc in range(2):
@@ -560,11 +561,10 @@ def tile_window_attention_t_kernel(tc, kv, q, mask, out):
             if s in sq_at:
                 scale_q(sq_at[s][0], sq_at[s][1], sq_at[s][2], 0, 32)
         mx(13, 1)
-        spread_r(14)
         exp_tile(62)
-        row_min(63)
         tr_x(59)
         exp_tile(63)
+        spread_r(14)
         quant_e(14)
         recip(15)
         tr_x(60)

from contextlib import ExitStack

import concourse.mybir as mybir
from concourse.masks import make_identity

F32 = mybir.dt.float32
BF16 = mybir.dt.bfloat16
U32 = mybir.dt.uint32
U8 = mybir.dt.uint8
FP8X4 = mybir.dt.float8_e4m3fn_x4
ALU = mybir.AluOpType
ACT = mybir.ActivationFunctionType
AX = mybir.AxisListType

P = 128
NKEY = 1024
NT = 64
FLOPS = 2 * 2 * 8 * 1024 * 1024 * 256

T_LAG = 5
E_BUFS = 5
U_BUFS = 5
PE_MASK = (2, 7, 12)
MT_SET = (4, 9, 14)
MT_LEAD = 2
MT_FIRST = 5
MT_FROM = 8
MT_V = ()
LAST_SPLIT = (2, 2)
GP_UNTIL = 52
DMA_INSTS = 7
D_QE = 6
D_RC = 6
D_MX = (8, 9)
D_M = (8, 9)
D_LAST = (3, 4, (7, 8), (99, 99))
D_MD5 = ((11, 12), (12, 13))
V_EVAC = (59,)
D_RD = 7
D_MD = ((11, 11), (15, 15))
D_VT = (0, 4)
D_QV = 5
D_SQ = (6, 10, 14, 18)
SQ0 = 4


def tile_window_attention_t_kernel(tc, kv, q, mask, out):
    nc = tc.nc
    with ExitStack() as ctx:
        const = ctx.enter_context(tc.tile_pool(name="const", bufs=1))
        maskp = ctx.enter_context(tc.tile_pool(name="maskp", bufs=1))
        inp = ctx.enter_context(tc.tile_pool(name="inp", bufs=2))
        work = ctx.enter_context(tc.tile_pool(name="work", bufs=2))
        ps_s = ctx.enter_context(tc.psum_pool(name="ps_s", bufs=2))
        ps_t = ctx.enter_context(tc.psum_pool(name="ps_t", bufs=3))
        ps_o = ctx.enter_context(tc.psum_pool(name="ps_o", bufs=1))
        ctx.enter_context(tc.manual_schedule())

        ident_bf = const.tile([P, P], BF16, name="ident_bf")
        make_identity(nc, ident_bf[:])
        ident_f = const.tile([P, P], F32, name="ident_f")
        make_identity(nc, ident_f[:])
        identm = const.tile([P, P], BF16, name="identm")
        nc.vector.tensor_scalar_mul(out=identm[:], in0=ident_bf[:], scalar1=-1.0)

        mask_sb = [maskp.tile([P, 8, NKEY], BF16, name="mask%d" % v) for v in range(2)]
        rpad = [const.tile([P, P], F32, name="rpad%d" % k) for k in range(2)]

        groups = [(4 * h, 4) for h in range(15)]
        first = 60
        for n in LAST_SPLIT:
            groups.append((first, n))
            first += n
        group_of = {}
        for gi, (g0, gn) in enumerate(groups):
            for i in range(g0, g0 + gn):
                group_of[i] = gi
        by_last = {}
        for gi, (g0, gn) in enumerate(groups):
            by_last[g0 + gn - 1] = gi

        kraw = {}
        qd = {}
        qs = {}
        vd = {}
        oa = {}
        vcode = {}
        vscale = {}
        gvt = {}
        st = {}
        ut = {}
        nmt = {}
        nm2t = {}
        et = {}
        xtt = {}
        grp = {}
        rst = {}
        rt = {}
        rsb = {}
        rpt = {}
        rsi = {}
        rbt = {}
        ecode = {}
        escale = {}
        ot = {}
        mt = {}

        def half(nh):
            return slice(nh * 512, (nh + 1) * 512)

        def chan0(pr, cc):
            return (pr % 2) * 256 + cc * P

        def load_rows(t, src, pr, cc, h0, h1):
            c0 = chan0(pr, cc)
            nc.sync.dma_start(
                out=t[:, h0 * 64:h1 * 64],
                in_=src[c0:c0 + P, h0:h1, :].rearrange("c h w -> c (h w)"),
            )

        def load_k(pr, cc, h0, h1):
            load_rows(kraw[(pr, cc)], kv[0, pr // 2], pr, cc, h0, h1)

        def load_q(pr, cc, h0, h1):
            load_rows(qd[(pr, cc)], q[pr // 2], pr, cc, h0, h1)

        def load_v(inst, cc):
            pr, v = inst // 2, inst % 2
            c0 = chan0(pr, cc)
            vd[(inst, cc)] = inp.tile([P, NKEY], BF16, name="vd%d%d" % (cc, v), tag="vd%d%d" % (cc, v))
            nc.sync.dma_start(
                out=vd[(inst, cc)][:].rearrange("c (h w) -> c h w", w=32),
                in_=kv[1, pr // 2, c0:c0 + P, :, v * 32:(v + 1) * 32],
            )

        def scale_q(pr, cc, v, h0, h1):
            qview = qd[(pr, cc)][:].rearrange("c (h v w) -> c h v w", v=2, w=32)
            nc.gpsimd.tensor_scalar(
                out=qs[(pr, cc, v)][:, h0 * 32:h1 * 32].rearrange("c (h w) -> c h w", w=32),
                in0=qview[:, h0:h1, v, :],
                scalar1=-1.0 / 16.0,
                scalar2=0.0,
                op0=ALU.mult,
                op1=ALU.add,
            )

        def load_mask(v, t0, n):
            nc.sync.dma_start(
                out=mask_sb[v][:, t0:t0 + n, :],
                in_=mask[v, t0 * P:(t0 + n) * P, :].rearrange("(t p) k -> p t k", p=P),
            )

        def load_mask_half(nh):
            nc.sync.dma_start(
                out=mask_sb[0][:, 0:2, half(nh)],
                in_=mask[0, 0:2 * P, half(nh)].rearrange("(t p) k -> p t k", p=P),
            )

        def load_pair(pr):
            for cc in range(2):
                kraw[(pr, cc)] = inp.tile([P, 2048], BF16, name="kraw%d" % cc, tag="kraw%d" % cc)
                qd[(pr, cc)] = inp.tile([P, 2048], BF16, name="qd%d" % cc, tag="qd%d" % cc)
                for v in range(2):
                    qs[(pr, cc, v)] = inp.tile([P, NKEY], BF16, name="qs%d%d" % (cc, v), tag="qs%d%d" % (cc, v))
            if pr == 0:
                for cc in range(2):
                    load_q(pr, cc, 0, 8)
                    scale_q(pr, cc, 0, 0, 8)
                for cc in range(2):
                    load_k(pr, cc, 0, 16)
                load_mask_half(0)
                for cc in range(2):
                    load_k(pr, cc, 16, 32)
                load_mask_half(1)
                for cc in range(2):
                    load_q(pr, cc, 8, 16)
                    scale_q(pr, cc, 0, 8, 16)
                load_mask(0, 2, 2)
                for cc in range(2):
                    load_q(pr, cc, 16, 32)
                    scale_q(pr, cc, 0, 16, 32)
                load_mask(0, 4, 4)
                for cc in range(2):
                    load_v(0, cc)
                load_mask(1, 0, 4)
                for cc in range(2):
                    load_v(1, cc)
                load_mask(1, 4, 4)
            else:
                for cc in range(2):
                    load_k(pr, cc, 0, 32)
                for cc in range(2):
                    load_q(pr, cc, 0, 32)
                for v in range(2):
                    for cc in range(2):
                        load_v(2 * pr + v, cc)

        def where(i):
            inst = i // 8
            return inst // 2, inst % 2, i % 8

        def on_pe(i, nh):
            return i % 16 in PE_MASK or i == NT - 1 and nh == 1

        def on_mt(i):
            return i >= MT_FROM and i % 16 in MT_SET

        def in_psum(i, nh):
            return on_pe(i, nh) or on_mt(i)

        def perm(ap):
            return ap.rearrange("q (p u e) -> q u p e", u=2, e=2)

        def flat(ap):
            return ap.rearrange("q (u p e) -> q u p e", u=2, e=2)

        def scores(i, nh, between=None):
            pr, v, qt = where(i)
            s_nh = ps_s.tile([P, 512], F32, name="s%d" % nh, tag="s%d" % nh)
            st[(i, nh)] = s_nh
            for cc in range(2):
                if cc == 1 and between is not None:
                    between()
                kview = kraw[(pr, cc)][:].rearrange("c (h v w) -> c h v w", v=2, w=32)
                nc.tensor.matmul(
                    out=s_nh[:].rearrange("p (h w) -> p h w", w=32),
                    lhsT=qs[(pr, cc, v)][:, qt * P:(qt + 1) * P],
                    rhs=kview[:, nh * 16:(nh + 1) * 16, v, :],
                    start=(cc == 0),
                    stop=(cc == 1 and not in_psum(i, nh)),
                )
            if on_mt(i):
                for kb in range(4):
                    nc.tensor.matmul(
                        out=s_nh[:, kb * P:(kb + 1) * P], lhsT=mt[i % 16][:, 4 * nh + kb, :], rhs=ident_f[:],
                        is_transpose=True, start=False, stop=(kb == 3),
                    )
            if on_pe(i, nh):
                nc.tensor.matmul(out=s_nh[:], lhsT=identm[:], rhs=mask_sb[v][:, qt, half(nh)], start=False, stop=True)

        def transposes(i, part):
            if part == 0:
                xtt[i] = ps_t.tile([P, 4, P], F32, name="xt", tag="t")
            ewords = et[i][:].bitcast(F32)
            for kb in range(2 * part, 2 * part + 2):
                nc.tensor.transpose(out=xtt[i][:, kb, :], in_=ewords[:, kb * P:(kb + 1) * P], identity=ident_f[:])

        def leave_psum(i, nh):
            pr, v, qt = where(i)
            if nh == 0:
                ut[i] = work.tile([P, NKEY], F32, name="u", tag="u", bufs=U_BUFS)
                if in_psum(i, 1):
                    nm2t[i] = work.tile([P, 1], F32, name="nm2", tag="nm2", bufs=2)
            u = ut[i]
            if in_psum(i, nh) and nh == 1:
                nmt[i] = work.tile([P, 1], F32, name="nm", tag="nm", bufs=6)
                nc.vector.tensor_scalar(
                    out=flat(u[:, half(nh)]), in0=perm(st[(i, nh)][:]), scalar1=1.0, scalar2=nm2t[i][:],
                    op0=ALU.mult, op1=ALU.min, accum_out=nmt[i][:],
                )
            elif in_psum(i, nh):
                nc.vector.tensor_scalar(
                    out=flat(u[:, half(nh)]), in0=perm(st[(i, nh)][:]), scalar1=1.0, scalar2=None,
                    op0=ALU.mult, op1=ALU.min, accum_out=nm2t[i][:],
                )
            else:
                nc.vector.tensor_tensor(
                    out=flat(u[:, half(nh)]), in0=perm(st[(i, nh)][:]), in1=perm(mask_sb[v][:, qt, half(nh)]),
                    op=ALU.subtract,
                )
                if nh == 0 and in_psum(i, 1):
                    nc.vector.tensor_reduce(out=nm2t[i][:], in_=u[:, half(0)], axis=AX.X, op=ALU.min)

        def build_mt(k):
            v, qt = k // 8, k % 8
            pt = ps_t.tile([P, 8, P], BF16, name="pm", tag="t")
            for kb in range(8):
                nc.tensor.transpose(out=pt[:, kb, :], in_=mask_sb[v][:, qt, kb * P:(kb + 1) * P], identity=ident_bf[:])
            mt[k] = maskp.tile([P, 8, P], F32, name="mt%d" % k)
            if k in MT_V:
                nc.vector.tensor_scalar_mul(out=mt[k][:], in0=pt[:], scalar1=-1.0)
            else:
                nc.scalar.activation(out=mt[k][:], in_=pt[:], func=ACT.Copy, scale=-1.0)

        def row_min(i):
            if in_psum(i, 1):
                return
            nm = work.tile([P, 1], F32, name="nm", tag="nm", bufs=6)
            nmt[i] = nm
            nc.vector.tensor_reduce(out=nm[:], in_=ut[i][:], axis=AX.X, op=ALU.min)

        def by_dma(i):
            return i // 8 < DMA_INSTS

        def exp_tile(i):
            gi = group_of[i]
            g0, gn = groups[gi]
            if by_dma(i):
                if i % 8 == 0:
                    rsi[i // 8] = work.tile([P, 8], F32, name="rsi", tag="rsi", bufs=2)
                col = rsi[i // 8][:, i % 8:i % 8 + 1]
            else:
                if i == g0:
                    rst[gi] = work.tile([P, 4], F32, name="rs", tag="rs", bufs=4)
                col = rst[gi][:, i - g0:i - g0 + 1]
            e = work.tile([P, NKEY], BF16, name="e", tag="e", bufs=E_BUFS)
            et[i] = e
            nc.scalar.activation(out=e[:], in_=ut[i][:], func=ACT.Exp, bias=nmt[i][:], scale=-1.0, accum_out=col)

        def evac_tile(i):
            gi = group_of[i]
            g0, gn = groups[gi]
            jj = i - g0
            if jj == 0:
                grp[gi] = work.tile([P, 2, gn * P, 4], BF16, name="grp", tag="grp", bufs=2, align_bytes=64)
            gw = grp[gi][:].rearrange("p g n t -> p (g n t)").bitcast(F32).rearrange("p (g n u) -> p g n u", g=2, u=2)
            ew = gw[:, :, jj * P:(jj + 1) * P, :]
            xw = xtt[i][:].rearrange("p (g u) n -> p g n u", u=2)
            if i in V_EVAC:
                nc.vector.tensor_copy(out=ew, in_=xw)
            else:
                nc.scalar.copy(out=ew, in_=xw)

        def vpath_pe(inst, cc):
            if inst not in gvt:
                gvt[inst] = work.tile([P, 2, 256, 4], BF16, name="gv", tag="gv", bufs=2, align_bytes=64)
            gwords = gvt[inst][:].rearrange("p g c t -> p (g c t)").bitcast(F32).rearrange("p (g c u) -> p g c u", g=2, u=2)
            vwords = vd[(inst, cc)][:].bitcast(F32)
            vt = ps_t.tile([P, 4, P], F32, name="vt", tag="t")
            for g in range(2):
                for uu in range(2):
                    nc.tensor.transpose(out=vt[:, 2 * g + uu, :], in_=vwords[:, 256 * g + uu:256 * (g + 1):2], identity=ident_f[:])
            nc.scalar.copy(
                out=gwords[:, :, cc * P:(cc + 1) * P, :],
                in_=vt[:].rearrange("p (g u) c -> p g c u", u=2),
            )

        def vpath_q(inst):
            vcode[inst] = work.tile([P, 512], U32, name="vcode", tag="vcode", bufs=2, align_bytes=64)
            vscale[inst] = work.tile([P, 512], U8, name="vscale", tag="vscale", bufs=2, align_bytes=64)
            nc.vector.quantize_mx(
                out=vcode[inst][:].bitcast(FP8X4),
                scales=vscale[inst][:],
                in_=gvt[inst][:].rearrange("p g c t -> p (g c t)"),
            )

        def recip(gi):
            g0, gn = groups[gi]
            rt[gi] = work.tile([P, 4], F32, name="r", tag="r", bufs=3)
            nc.vector.reciprocal(out=rt[gi][:, 0:gn], in_=rst[gi][:, 0:gn])

        def quant_e(gi):
            g0, gn = groups[gi]
            ecode[gi] = work.tile([P, 2 * gn * P], U32, name="ecode", tag="ecode", bufs=2, align_bytes=64)
            escale[gi] = work.tile([P, 2 * gn * P], U8, name="escale", tag="escale", bufs=2, align_bytes=64)
            nc.vector.quantize_mx(
                out=ecode[gi][:].bitcast(FP8X4),
                scales=escale[gi][:],
                in_=grp[gi][:].rearrange("p g n t -> p (g n t)"),
            )

        def spread_r(gi):
            g0, gn = groups[gi]
            if g0 >= 56:
                rp = ps_s.tile([P, gn * P], F32, name="rp%d" % (gi % 2), tag="s%d" % (gi % 2))
            else:
                rp = ps_t.tile([P, gn * P], F32, name="rp", tag="t")
            for jj in range(gn):
                nc.tensor.transpose(
                    out=rp[:, jj * P:(jj + 1) * P],
                    in_=rt[gi][:, jj:jj + 1].to_broadcast([P, P]),
                    identity=ident_f[:],
                )
            rsb[gi] = work.tile([P, gn * P], F32, name="rsb", tag="rsb", bufs=3)
            nc.scalar.copy(out=rsb[gi][:], in_=rp[:])

        def sums_recip(inst):
            nc.vector.reciprocal(out=rpad[inst % 2][:, 0:8], in_=rsi[inst][:])

        def sums_t(inst):
            rpt[inst] = ps_t.tile([P, P], F32, name="rpt", tag="t")
            nc.tensor.transpose(out=rpt[inst][:], in_=rpad[inst % 2][:], identity=ident_f[:])

        def sums_spread(inst):
            rrow = work.tile([8, P], F32, name="rrow", tag="rrow", bufs=2)
            nc.scalar.copy(out=rrow[:], in_=rpt[inst][0:8, :])
            h0 = (inst % 2) * 16
            rows = out[1, 511 - inst // 2, h0:h0 + 16, :]
            nc.sync.dma_start(out=rows.rearrange("(t a) w -> t (a w)", a=2), in_=rrow[:])
            rbt[inst] = work.tile([P, NKEY], F32, name="rb", tag="rb", bufs=2)
            nc.sync.dma_start(out=rbt[inst][:], in_=rows.rearrange("h w -> (h w)").partition_broadcast(P))

        def mx(gi, cc):
            g0, gn = groups[gi]
            inst = g0 // 8
            w = gn * P
            if g0 + cc >= 53:
                o_t = ps_s.tile([P, w], F32, name="os%d" % cc, tag="s%d" % cc)
            else:
                o_t = ps_o.tile([P, w], F32, name="o", tag="o")
            ot[(gi, cc)] = o_t[:]
            for g in range(2):
                w0 = g * 256 + cc * P
                nc.tensor.matmul_mx(
                    out=ot[(gi, cc)],
                    lhsT=vcode[inst][:, w0:w0 + P].bitcast(FP8X4),
                    lhsT_scale=vscale[inst][:, w0:w0 + P],
                    rhs=ecode[gi][:, g * w:(g + 1) * w].bitcast(FP8X4),
                    rhs_scale=escale[gi][:, g * w:(g + 1) * w],
                    start=(g == 0),
                    stop=(g == 1),
                )

        def pace(i):
            hold = work.tile([P, 1], F32, name="hold", tag="hold", bufs=2)
            nc.gpsimd.tensor_copy(out=hold[:], in_=ut[i][:, 0:1])

        def on_gp(gi):
            return groups[gi][0] < GP_UNTIL

        def oa_part(gi, cc):
            g0, gn = groups[gi]
            pr, v, qt = where(g0)
            if (pr, cc) not in oa:
                oa[(pr, cc)] = work.tile([P, 32, 2, 32], F32, name="oa%d" % cc, tag="oa%d" % cc, bufs=2)
            return oa[(pr, cc)][:, qt * 4:(qt + gn) * 4, v, :]

        def o_out(gi, cc):
            nc.scalar.copy(out=oa_part(gi, cc), in_=ot[(gi, cc)].rearrange("p (h w) -> p h w", w=32))

        def tr_x(i):
            transposes(i, 0)
            transposes(i, 1)
            evac_tile(i)

        def norm_store(gi, cc):
            g0, gn = groups[gi]
            pr, v, qt = where(g0)
            h0, h1 = qt * 4, (qt + gn) * 4
            part = oa_part(gi, cc)
            if by_dma(g0):
                r = rbt[g0 // 8][:, qt * P:(qt + gn) * P]
            else:
                r = rsb[gi][:]
            r = r.rearrange("p (h w) -> p h w", w=32)
            if on_gp(gi):
                nc.gpsimd.tensor_tensor(out=part, in0=part, in1=r, op=ALU.mult)
            else:
                nc.vector.tensor_tensor(
                    out=part, in0=ot[(gi, cc)].rearrange("p (h w) -> p h w", w=32), in1=r, op=ALU.mult,
                )
            if v == 1:
                c0 = chan0(pr, cc)
                nc.sync.dma_start(
                    out=out[pr // 2, c0:c0 + P, h0:h1, :].rearrange("c h w -> c (h w)"),
                    in_=oa[(pr, cc)][:, h0:h1, :, :].rearrange("c h v w -> c (h v w)"),
                )

        def grp_at(s, d):
            return by_last.get(s - d)

        def half_at(s, d, cc):
            gi = by_last.get(s - d[cc])
            if gi is not None and groups[gi][0] >= 60:
                gi = None
            if gi is None:
                gl = by_last.get(s - d[0])
                if gl is not None and groups[gl][0] >= 60:
                    gi = gl
            return gi

        vt_at = {}
        vq_at = {}
        for inst in range(8):
            for cc in range(2):
                vt_at[(max(8 * inst + D_VT[cc], 6), cc)] = inst
            vq_at[max(8 * inst + D_QV, 8)] = inst

        sq_at = {}
        for pr in range(1, 4):
            for k in range(4):
                sq_at[16 * (pr - 1) + D_SQ[k]] = (pr, k % 2, k // 2)
        sq_at[SQ0] = (0, 0, 1)
        sq_at[SQ0 + 1] = (0, 1, 1)

        st_at = {}
        sr_at = {}
        md_at = {}
        for inst in range(DMA_INSTS):
            d_rc, d_rd, d_md = (D_LAST[0], D_LAST[1], D_LAST[2:]) if inst == 6 else (D_RC, D_RD, D_MD5 if inst == 5 else D_MD)
            st_at[8 * inst + 7 + d_rd] = inst
            if inst < 6:
                sr_at[8 * inst + 7 + d_rc] = inst
            for k in range(2):
                for cc in range(2):
                    md_at.setdefault(8 * inst + 7 + d_md[k][cc], []).append((2 * inst + k, cc))

        load_pair(0)
        for t in rpad:
            nc.gpsimd.memset(t[:], 0.0)
        for s in range(NT):
            if s % 16 == 0 and s // 16 + 1 < 4:
                load_pair(s // 16 + 1)
            j = s - T_LAG
            if s != 1:
                scores(s, 0)
            if s == 0:
                scores(1, 0)
            due = [(half_at(s, D_MX, cc), cc) for cc in range(2) if half_at(s, D_MX, cc) is not None]

            def sums():
                for gi, cc in due:
                    mx(gi, cc)

            scores(s, 1, sums)
            for gi, cc in due:
                if on_gp(gi):
                    o_out(gi, cc)
            if j >= 0:
                transposes(j, 0)
                transposes(j, 1)
                evac_tile(j)
            for cc in range(2):
                if (s, cc) in vt_at:
                    vpath_pe(vt_at[(s, cc)], cc)
            if s in st_at:
                sums_t(st_at[s])
                sums_spread(st_at[s])
            if 0 <= s - 2 < NT:
                exp_tile(s - 2)
            if s == 2:
                row_min(1)
            if s == 55 + D_LAST[0]:
                sums_recip(6)
            if s != 1:
                leave_psum(s, 0)
            if s == 62:
                recip(14)
            if s == 0:
                leave_psum(1, 0)
            if s >= 1 and s != 2:
                row_min(s - 1)
            leave_psum(s, 1)
            if s in vq_at:
                vpath_q(vq_at[s])
            if s in sr_at:
                sums_recip(sr_at[s])
            if grp_at(s, D_QE) is not None:
                quant_e(grp_at(s, D_QE))
            for cc in range(2):
                gi = half_at(s, D_M, cc)
                if gi is not None and not by_dma(groups[gi][0]):
                    norm_store(gi, cc)
            if s > 2 and (s in md_at or s in sq_at):
                pace(s)
            for gi, cc in md_at.get(s, []):
                norm_store(gi, cc)
            for k in MT_SET:
                if s == max(k - MT_LEAD, MT_FIRST):
                    build_mt(k)
            if s in sq_at:
                scale_q(sq_at[s][0], sq_at[s][1], sq_at[s][2], 0, 32)
        mx(13, 1)
        exp_tile(62)
        tr_x(59)
        exp_tile(63)
        spread_r(14)
        quant_e(14)
        recip(15)
        tr_x(60)
        tr_x(61)
        norm_store(13, 0)
        tr_x(62)
        mx(14, 0)
        mx(14, 1)
        tr_x(63)
        norm_store(13, 1)
        norm_store(14, 0)
        norm_store(14, 1)
        quant_e(15)
        recip(16)
        spread_r(15)
        mx(15, 0)
        mx(15, 1)
        quant_e(16)
        spread_r(16)
        norm_store(15, 0)
        norm_store(15, 1)
        mx(16, 0)
        mx(16, 1)
        norm_store(16, 0)
        norm_store(16, 1)
